import numpy as np
import ml_dtypes


def mxq(x, axis, fmt="e4m3"):
    dtype, down = {"e4m3": (ml_dtypes.float8_e4m3fn, 7), "e5m2": (ml_dtypes.float8_e5m2, 14)}[fmt]
    v = np.moveaxis(np.asarray(x, np.float32).astype(ml_dtypes.bfloat16).astype(np.float64), axis, -1)
    blocks = v.reshape(v.shape[:-1] + (-1, 32))
    amax = np.abs(blocks).max(-1, keepdims=True)
    byte = np.maximum(np.where(amax > 0, np.frexp(amax)[1] - 1 + 127, 0) - down, 1)
    scale = np.exp2(byte - 127.0)
    codes = (blocks / scale).astype(np.float32).astype(dtype).astype(np.float64)
    return np.moveaxis((codes * scale).reshape(v.shape), -1, axis)


WIDE = False


def mx_kscale(k):
    if not WIDE:
        return np.ones(k)
    levels = np.array([10, -10, 5, -5, 0])
    a = np.random.permutation(np.resize(levels, k // 512 * 4)).reshape(k // 512, 4)
    idx = np.arange(k)
    return np.exp2(a[idx // 512, idx % 128 // 32])


BF16 = ml_dtypes.bfloat16


def bf(x):
    return np.asarray(x, np.float32).astype(BF16)


def f64(x):
    return np.asarray(x).astype(np.float64)


B, N, VF_D, HID_D, EMB_D = 256, 512, 4096, 2048, 512
C = 6.0 / np.sqrt(EMB_D)


def _partial_order_sim(hypers, hypos):
    act = np.maximum(hypers - hypos, 0.0)
    return -np.sqrt(np.sum(act * act, axis=-1))


def setup_inputs():
    s, t = mx_kscale(VF_D), mx_kscale(HID_D)
    return {"vfs": bf(np.random.standard_normal((B, VF_D)) * s),
            "p_lfs": bf(np.random.standard_normal((B, EMB_D)) * 2.0 * C),
            "n_lfs": bf(np.random.standard_normal((N, EMB_D)) * C),
            "W_hidden": bf(np.random.standard_normal((HID_D, VF_D)) / np.sqrt(VF_D) / s[None, :] * t[:, None]),
            "b_hidden": bf(np.random.standard_normal(HID_D) * 0.5 * t),
            "W_embed": bf(np.random.standard_normal((EMB_D, HID_D)) * C / np.sqrt(HID_D) / t[None, :]),
            "b_embed": bf(np.random.standard_normal(EMB_D) * 0.5 * C)}


def reference(vfs, p_lfs, n_lfs, W_hidden, b_hidden, W_embed, b_embed):
    vf_hidden = (mxq(f64(vfs), 1, "e4m3") @ mxq(f64(W_hidden), 1, "e4m3").T) + f64(b_hidden)
    vf_emb = (mxq(vf_hidden, 1, "e4m3") @ mxq(f64(W_embed), 1, "e4m3").T) + f64(b_embed)
    p_scores = _partial_order_sim(f64(p_lfs), vf_emb)
    n_scores = np.stack([_partial_order_sim(nl[None, :], vf_emb) for nl in f64(n_lfs)], axis=1)
    return np.concatenate([p_scores[:, None], n_scores], axis=1)

@@ -1,0 +1,298 @@
+from contextlib import ExitStack
+
+import concourse.mybir as mybir
+from concourse.masks import make_identity
+
+F32 = mybir.dt.float32
+BF16 = mybir.dt.bfloat16
+U32 = mybir.dt.uint32
+U8 = mybir.dt.uint8
+FP8X4 = mybir.dt.float8_e4m3fn_x4
+ALU = mybir.AluOpType
+ACT = mybir.ActivationFunctionType
+
+P = 128
+B, NNEG, VF, HID, EMB = 256, 512, 4096, 2048, 512
+FLOPS = 2 * B * VF * HID + 2 * B * HID * EMB + 4 * B * (NNEG + 1) * EMB
+
+R_BUFS = 4
+JUNK_BUFS = 4
+
+
+def tile_hypernymvisual_acc_kernel(tc, vfs, p_lfs, n_lfs, W_hidden, b_hidden, W_embed, b_embed, out):
+    nc = tc.nc
+    with ExitStack() as ctx:
+        keep = ctx.enter_context(tc.tile_pool(name="keep", bufs=1))
+        ident_f = keep.tile([P, P], F32)
+        make_identity(nc, ident_f[:])
+        ident_b = keep.tile([P, P], BF16)
+        make_identity(nc, ident_b[:])
+        nT = keep.tile([P, 4, NNEG], F32)
+        pT = keep.tile([P, 4, B], F32)
+        eT = keep.tile([P, 4, B], F32)
+        bias = keep.tile([P, 32], F32)
+        one = keep.tile([P, 1], F32)
+        nc.vector.memset(one[:], 1.0)
+        warm = keep.tile([P, 1], F32)
+        nc.scalar.activation(out=warm[:], in_=one[:], func=ACT.Sqrt)
+
+        with ExitStack() as mx:
+            fix = mx.enter_context(tc.tile_pool(name="fix", bufs=1))
+            raws = mx.enter_context(tc.tile_pool(name="raws", bufs=6))
+            work = mx.enter_context(tc.tile_pool(name="work", bufs=2))
+            ps_t = mx.enter_context(tc.psum_pool(name="ps_t", bufs=5))
+            ps_a = mx.enter_context(tc.psum_pool(name="ps_a", bufs=2))
+
+            copy_turn = [0]
+
+            def copy_out(dst, src):
+                if copy_turn[0] % 2 == 0:
+                    nc.vector.tensor_copy(out=dst, in_=src)
+                else:
+                    nc.scalar.copy(out=dst, in_=src)
+                copy_turn[0] += 1
+
+            vraw = []
+            for bc in range(2):
+                t = fix.tile([P, VF], BF16, name="vraw%d" % bc)
+                nc.sync.dma_start(out=t[:], in_=vfs[bc * P : (bc + 1) * P, :])
+                vraw.append(t)
+            brow = fix.tile([P, P], BF16)
+            nc.vector.memset(brow[:], 0.0)
+            nc.scalar.dma_start(out=brow[0:16, :], in_=b_hidden.rearrange("(r c) -> r c", c=P))
+            nc.scalar.dma_start(out=brow[16:20, :], in_=b_embed.rearrange("(r c) -> r c", c=P))
+            weraw = fix.tile([P, 4 * HID], BF16)
+            nraw = fix.tile([P, 4 * EMB], BF16)
+            praw = fix.tile([P, 2 * EMB], BF16)
+
+            wraws = []
+
+            def load_w(hc):
+                t = raws.tile([P, VF], BF16, name="wraw", tag="wraw")
+                nc.sync.dma_start(out=t[:], in_=W_hidden[hc * P : (hc + 1) * P, :])
+                wraws.append(t)
+
+            for hc in range(3):
+                load_w(hc)
+            nc.sync.dma_start(
+                out=weraw[:].rearrange("p (c k) -> p c k", c=4), in_=W_embed.rearrange("(c p) k -> p c k", p=P)
+            )
+            nc.sync.dma_start(
+                out=nraw[:].rearrange("p (c k) -> p c k", c=4), in_=n_lfs.rearrange("(c p) k -> p c k", p=P)
+            )
+            nc.sync.dma_start(
+                out=praw[:].rearrange("p (c k) -> p c k", c=2), in_=p_lfs.rearrange("(c p) k -> p c k", p=P)
+            )
+
+            bt = ps_t.tile([P, P], BF16, tag="xt")
+            nc.tensor.transpose(out=bt[:], in_=brow[:], identity=ident_b[:])
+            nc.vector.tensor_copy(out=bias[:], in_=bt[:, 0:32])
+
+            vgrp = fix.tile([P, 8 * B * 4], BF16, align_bytes=64)
+            vgrp_w = vgrp[:].bitcast(F32).rearrange("p (g r u) -> p g r u", g=8, r=B, u=2)
+            vcodes = fix.tile([P, 8 * B], U32, align_bytes=64)
+            vscales = fix.tile([P, 8 * B], U8, align_bytes=64)
+            for bc in range(2):
+                words = vraw[bc][:].bitcast(F32)
+                for q in range(4):
+                    xt = ps_t.tile([P, 2, 2, P], F32, tag="xt")
+                    for gg in range(2):
+                        for u in range(2):
+                            lo = 256 * (2 * q + gg) + P * u
+                            nc.tensor.transpose(out=xt[:, gg, u, :], in_=words[:, lo : lo + P], identity=ident_f[:])
+                    copy_out(
+                        vgrp_w[:, 2 * q : 2 * q + 2, bc * P : (bc + 1) * P, :],
+                        xt[:].rearrange("p g u r -> p g r u"),
+                    )
+            for h in range(2):
+                nc.vector.quantize_mx(
+                    out=vcodes[:, 1024 * h : 1024 * (h + 1)].bitcast(FP8X4),
+                    scales=vscales[:, 1024 * h : 1024 * (h + 1)],
+                    in_=vgrp[:, 4096 * h : 4096 * (h + 1)],
+                )
+
+            hgrp = fix.tile([P, 4 * B * 4], BF16, align_bytes=64)
+            hgrp_v = hgrp[:].rearrange("p (g b t) -> p g b t", g=4, b=B, t=4)
+            hcodes = fix.tile([P, 4 * B], U32, align_bytes=64)
+            hscales = fix.tile([P, 4 * B], U8, align_bytes=64)
+            egrp = fix.tile([P, 4 * EMB * 4], BF16, align_bytes=64)
+            egrp_v = egrp[:].rearrange("p (g d t) -> p g d t", g=4, d=EMB, t=4)
+            ecodes = fix.tile([P, 4 * EMB], U32, align_bytes=64)
+            escales = fix.tile([P, 4 * EMB], U8, align_bytes=64)
+
+            def side_work():
+                for dc in range(4):
+                    for gh in range(2):
+                        xb = ps_t.tile([P, 2, 4, P], BF16, tag="xt")
+                        for gg in range(2):
+                            for t in range(4):
+                                lo = dc * HID + 512 * (2 * gh + gg) + P * t
+                                nc.tensor.transpose(out=xb[:, gg, t, :], in_=weraw[:, lo : lo + P], identity=ident_b[:])
+                        copy_out(
+                            egrp_v[:, 2 * gh : 2 * gh + 2, dc * P : (dc + 1) * P, :],
+                            xb[:].rearrange("p g t r -> p g r t"),
+                        )
+                for h in range(2):
+                    nc.vector.quantize_mx(
+                        out=ecodes[:, 1024 * h : 1024 * (h + 1)].bitcast(FP8X4),
+                        scales=escales[:, 1024 * h : 1024 * (h + 1)],
+                        in_=egrp[:, 4096 * h : 4096 * (h + 1)],
+                    )
+                for ch in range(2):
+                    nb = ps_t.tile([P, 2, NNEG], BF16, tag="xt")
+                    for cc in range(2):
+                        for jc in range(4):
+                            lo = jc * EMB + (2 * ch + cc) * P
+                            nc.tensor.transpose(
+                                out=nb[:, cc, jc * P : (jc + 1) * P], in_=nraw[:, lo : lo + P], identity=ident_b[:]
+                            )
+                    nc.vector.tensor_copy(out=nT[:, 2 * ch : 2 * ch + 2, :], in_=nb[:])
+                pb = ps_t.tile([P, 4, B], BF16, tag="xt")
+                for c in range(4):
+                    for ic in range(2):
+                        lo = ic * EMB + c * P
+                        nc.tensor.transpose(
+                            out=pb[:, c, ic * P : (ic + 1) * P], in_=praw[:, lo : lo + P], identity=ident_b[:]
+                        )
+                nc.vector.tensor_copy(out=pT[:], in_=pb[:])
+
+            for hc in range(16):
+                if hc + 3 < 16:
+                    load_w(hc + 3)
+                words = wraws[hc][:].bitcast(F32)
+                wgrp = work.tile([P, VF], BF16, align_bytes=64)
+                wgrp_w = wgrp[:].bitcast(F32).rearrange("p (g r u) -> p g r u", g=8, r=P, u=2)
+                for q in range(4):
+                    xt = ps_t.tile([P, 2, 2, P], F32, tag="xt")
+                    for gg in range(2):
+                        for u in range(2):
+                            lo = 256 * (2 * q + gg) + P * u
+                            nc.tensor.transpose(out=xt[:, gg, u, :], in_=words[:, lo : lo + P], identity=ident_f[:])
+                    copy_out(wgrp_w[:, 2 * q : 2 * q + 2, :, :], xt[:].rearrange("p g u r -> p g r u"))
+                wcodes = work.tile([P, 1024], U32, align_bytes=64)
+                wscales = work.tile([P, 1024], U8, align_bytes=64)
+                nc.vector.quantize_mx(out=wcodes[:].bitcast(FP8X4), scales=wscales[:], in_=wgrp[:])
+                acc = ps_a.tile([P, B], F32, tag="acc")
+                for g in range(8):
+                    nc.tensor.matmul_mx(
+                        out=acc[:],
+                        lhsT=wcodes[:, P * g : P * (g + 1)].bitcast(FP8X4),
+                        lhsT_scale=wscales[:, P * g : P * (g + 1)],
+                        rhs=vcodes[:, B * g : B * (g + 1)].bitcast(FP8X4),
+                        rhs_scale=vscales[:, B * g : B * (g + 1)],
+                        start=(g == 0),
+                        stop=(g == 7),
+                    )
+                g2, t = hc // 4, hc % 4
+                nc.scalar.activation(
+                    out=hgrp_v[:, g2, :, t], in_=acc[:], func=ACT.Identity, bias=bias[:, hc : hc + 1], scale=1.0
+                )
+                if t == 3:
+                    nc.vector.quantize_mx(
+                        out=hcodes[:, B * g2 : B * (g2 + 1)].bitcast(FP8X4),
+                        scales=hscales[:, B * g2 : B * (g2 + 1)],
+                        in_=hgrp[:, 4 * B * g2 : 4 * B * (g2 + 1)],
+                    )
+                if hc == 5:
+                    side_work()
+
+            for dc in range(4):
+                acc = ps_a.tile([P, B], F32, tag="acc")
+                for g2 in range(4):
+                    lo = EMB * g2 + P * dc
+                    nc.tensor.matmul_mx(
+                        out=acc[:],
+                        lhsT=ecodes[:, lo : lo + P].bitcast(FP8X4),
+                        lhsT_scale=escales[:, lo : lo + P],
+                        rhs=hcodes[:, B * g2 : B * (g2 + 1)].bitcast(FP8X4),
+                        rhs_scale=hscales[:, B * g2 : B * (g2 + 1)],
+                        start=(g2 == 0),
+                        stop=(g2 == 3),
+                    )
+                nc.scalar.activation(
+                    out=eT[:, dc, :], in_=acc[:], func=ACT.Identity, bias=bias[:, 16 + dc : 17 + dc], scale=1.0
+                )
+
+        fin = ctx.enter_context(tc.tile_pool(name="fin", bufs=1))
+        rpool = ctx.enter_context(tc.tile_pool(name="rpool", bufs=R_BUFS))
+        jpool = ctx.enter_context(tc.tile_pool(name="jpool", bufs=JUNK_BUFS))
+        banks = ctx.enter_context(tc.psum_pool(name="banks", bufs=8))
+
+        acc_s = fin.tile([P, 3, B], F32)
+        stats = fin.tile([P, B, 6], F32)
+        acc_p = fin.tile([P, 2], F32)
+
+        def square_sum(bank, dst):
+            junk = jpool.tile([P, EMB], F32, name="junk", tag="junk")
+            nc.scalar.activation(out=junk[:], in_=bank[:], func=ACT.Square, accum_out=dst)
+
+        rp = fin.tile([P, 4, B], F32)
+        nc.vector.tensor_tensor(out=rp[:], in0=pT[:], in1=eT[:], op=ALU.subtract)
+        nc.vector.tensor_scalar_max(out=rp[:], in0=rp[:], scalar1=0.0)
+        for ic in range(2):
+            bank = banks.tile([P, EMB], F32, name="bank", tag="bank")
+            for c in range(4):
+                nc.tensor.transpose(
+                    out=bank[:, c * P : (c + 1) * P], in_=rp[:, c, ic * P : (ic + 1) * P], identity=ident_f[:]
+                )
+            square_sum(bank, acc_p[:, ic : ic + 1])
+
+        r_tiles = {}
+        bank_tiles = {}
+
+        def relu_diff(i):
+            r = rpool.tile([P, 4, NNEG], F32, name="r", tag="r")
+            for c in range(4):
+                nc.vector.tensor_scalar(
+                    out=r[:, c, :],
+                    in0=nT[:, c, :],
+                    scalar1=eT[:, c, i : i + 1],
+                    scalar2=0.0,
+                    op0=ALU.subtract,
+                    op1=ALU.max,
+                )
+            r_tiles[i] = r
+
+        def turn(i):
+            r = r_tiles[i]
+            for jc in range(4):
+                bank = banks.tile([P, EMB], F32, name="bank", tag="bank")
+                for c in range(4):
+                    nc.tensor.transpose(
+                        out=bank[:, c * P : (c + 1) * P], in_=r[:, c, jc * P : (jc + 1) * P], identity=ident_f[:]
+                    )
+                bank_tiles[(i, jc)] = bank
+
+        def reduce_row(i):
+            for jc in range(3):
+                square_sum(bank_tiles[(i, jc)], acc_s[:, jc, i : i + 1])
+            nc.vector.bn_stats(out=stats[:, i, :], in_=bank_tiles[(i, 3)][:])
+
+        with tc.manual_schedule():
+            for s in range(B + 2):
+                if s < B:
+                    relu_diff(s)
+                if 0 <= s - 1 < B:
+                    turn(s - 1)
+                if 0 <= s - 2 < B:
+                    reduce_row(s - 2)
+
+        st = stats[:].rearrange("p i (h k) -> p i h k", h=2, k=3)
+        sq = fin.tile([P, B, 2], F32)
+        nc.vector.tensor_tensor(out=sq[:], in0=st[:, :, :, 1], in1=st[:, :, :, 1], op=ALU.mult)
+        nc.vector.scalar_tensor_tensor(
+            out=sq[:], in0=sq[:], scalar=float(EMB // 2), in1=st[:, :, :, 2], op0=ALU.mult, op1=ALU.add
+        )
+        acc_v = fin.tile([P, B], F32)
+        nc.vector.tensor_tensor(out=acc_v[:], in0=sq[:, :, 0], in1=sq[:, :, 1], op=ALU.add)
+
+        for ic in range(2):
+            bank = banks.tile([P, NNEG], F32, name="bank", tag="bank")
+            for jc in range(4):
+                src = acc_s[:, jc, ic * P : (ic + 1) * P] if jc < 3 else acc_v[:, ic * P : (ic + 1) * P]
+                nc.tensor.transpose(out=bank[:, jc * P : (jc + 1) * P], in_=src, identity=ident_f[:])
+            res = fin.tile([P, NNEG + 1], F32, name="res%d" % ic)
+            nc.scalar.activation(out=res[:, 0:1], in_=acc_p[:, ic : ic + 1], func=ACT.Sqrt)
+            nc.scalar.activation(out=res[:, 1 : NNEG + 1], in_=bank[:], func=ACT.Sqrt)
+            nc.vector.tensor_scalar_mul(out=res[:], in0=res[:], scalar1=-1.0)
+            nc.sync.dma_start(out=out[ic * P : (ic + 1) * P, :], in_=res[:])

@@ -15,13 +15,19 @@ P = 128
 B, NNEG, VF, HID, EMB = 256, 512, 4096, 2048, 512
 FLOPS = 2 * B * VF * HID + 2 * B * HID * EMB + 4 * B * (NNEG + 1) * EMB
 
+W_BUFS = 6
 R_BUFS = 4
 JUNK_BUFS = 4
+EXTRA_EVERY = 8
+EXTRA_AT = 3
+N_EXTRA = P // EXTRA_EVERY
+ROUND_ON_VECTOR = (3, 6, 7)
 
 
 def tile_hypernymvisual_acc_kernel(tc, vfs, p_lfs, n_lfs, W_hidden, b_hidden, W_embed, b_embed, out):
     nc = tc.nc
     with ExitStack() as ctx:
+        ctx.enter_context(tc.manual_schedule())
         keep = ctx.enter_context(tc.tile_pool(name="keep", bufs=1))
         ident_f = keep.tile([P, P], F32)
         make_identity(nc, ident_f[:])
@@ -31,40 +37,38 @@ def tile_hypernymvisual_acc_kernel(tc, vfs, p_lfs, n_lfs, W_hidden, b_hidden, W_
         pT = keep.tile([P, 4, B], F32)
         eT = keep.tile([P, 4, B], F32)
         bias = keep.tile([P, 32], F32)
+        acc_s = keep.tile([P, 3, B], F32)
+        nc.gpsimd.memset(acc_s[:], 0.0)
         one = keep.tile([P, 1], F32)
         nc.vector.memset(one[:], 1.0)
         warm = keep.tile([P, 1], F32)
-        nc.scalar.activation(out=warm[:], in_=one[:], func=ACT.Sqrt)
 
         with ExitStack() as mx:
             fix = mx.enter_context(tc.tile_pool(name="fix", bufs=1))
-            raws = mx.enter_context(tc.tile_pool(name="raws", bufs=6))
-            work = mx.enter_context(tc.tile_pool(name="work", bufs=2))
-            ps_t = mx.enter_context(tc.psum_pool(name="ps_t", bufs=5))
+            raws = mx.enter_context(tc.tile_pool(name="raws", bufs=W_BUFS))
+            work = mx.enter_context(tc.tile_pool(name="work", bufs=4))
+            ps_t = mx.enter_context(tc.psum_pool(name="ps_t", bufs=6))
             ps_a = mx.enter_context(tc.psum_pool(name="ps_a", bufs=2))
 
-            copy_turn = [0]
-
-            def copy_out(dst, src):
-                if copy_turn[0] % 2 == 0:
+            def copy_out(on_vector, dst, src):
+                if on_vector:
                     nc.vector.tensor_copy(out=dst, in_=src)
                 else:
                     nc.scalar.copy(out=dst, in_=src)
-                copy_turn[0] += 1
 
+            brow = fix.tile([P, P], BF16)
+            nc.vector.memset(brow[:], 0.0)
+            nc.scalar.dma_start(out=brow[0:16, :], in_=b_hidden.rearrange("(r c) -> r c", c=P))
+            nc.scalar.dma_start(out=brow[16:20, :], in_=b_embed.rearrange("(r c) -> r c", c=P))
+            nc.scalar.activation(out=warm[:], in_=one[:], func=ACT.Sqrt)
             vraw = []
             for bc in range(2):
                 t = fix.tile([P, VF], BF16, name="vraw%d" % bc)
                 nc.sync.dma_start(out=t[:], in_=vfs[bc * P : (bc + 1) * P, :])
                 vraw.append(t)
-            brow = fix.tile([P, P], BF16)
-            nc.vector.memset(brow[:], 0.0)
-            nc.scalar.dma_start(out=brow[0:16, :], in_=b_hidden.rearrange("(r c) -> r c", c=P))
-            nc.scalar.dma_start(out=brow[16:20, :], in_=b_embed.rearrange("(r c) -> r c", c=P))
             weraw = fix.tile([P, 4 * HID], BF16)
             nraw = fix.tile([P, 4 * EMB], BF16)
             praw = fix.tile([P, 2 * EMB], BF16)
-
             wraws = []
 
             def load_w(hc):
@@ -72,7 +76,7 @@ def tile_hypernymvisual_acc_kernel(tc, vfs, p_lfs, n_lfs, W_hidden, b_hidden, W_
                 nc.sync.dma_start(out=t[:], in_=W_hidden[hc * P : (hc + 1) * P, :])
                 wraws.append(t)
 
-            for hc in range(3):
+            for hc in range(4):
                 load_w(hc)
             nc.sync.dma_start(
                 out=weraw[:].rearrange("p (c k) -> p c k", c=4), in_=W_embed.rearrange("(c p) k -> p c k", p=P)
@@ -83,27 +87,32 @@ def tile_hypernymvisual_acc_kernel(tc, vfs, p_lfs, n_lfs, W_hidden, b_hidden, W_
             nc.sync.dma_start(
                 out=praw[:].rearrange("p (c k) -> p c k", c=2), in_=p_lfs.rearrange("(c p) k -> p c k", p=P)
             )
+            for hc in range(4, W_BUFS):
+                load_w(hc)
 
-            bt = ps_t.tile([P, P], BF16, tag="xt")
-            nc.tensor.transpose(out=bt[:], in_=brow[:], identity=ident_b[:])
-            nc.vector.tensor_copy(out=bias[:], in_=bt[:, 0:32])
+            def turn_words(words, dst_of_q, vector_banks, first_bank):
+                for q in range(4):
+                    xt = ps_t.tile([P, 2, 2, P], F32, name="xt", tag="xt")
+                    for gg in range(2):
+                        for u in range(2):
+                            lo = 256 * (2 * q + gg) + P * u
+                            nc.tensor.transpose(out=xt[:, gg, u, :], in_=words[:, lo : lo + P], identity=ident_f[:])
+                    copy_out((first_bank + q) in vector_banks, dst_of_q(q), xt[:].rearrange("p g u r -> p g r u"))
 
             vgrp = fix.tile([P, 8 * B * 4], BF16, align_bytes=64)
             vgrp_w = vgrp[:].bitcast(F32).rearrange("p (g r u) -> p g r u", g=8, r=B, u=2)
             vcodes = fix.tile([P, 8 * B], U32, align_bytes=64)
             vscales = fix.tile([P, 8 * B], U8, align_bytes=64)
             for bc in range(2):
-                words = vraw[bc][:].bitcast(F32)
-                for q in range(4):
-                    xt = ps_t.tile([P, 2, 2, P], F32, tag="xt")
-                    for gg in range(2):
-                        for u in range(2):
-                            lo = 256 * (2 * q + gg) + P * u
-                            nc.tensor.transpose(out=xt[:, gg, u, :], in_=words[:, lo : lo + P], identity=ident_f[:])
-                    copy_out(
-                        vgrp_w[:, 2 * q : 2 * q + 2, bc * P : (bc + 1) * P, :],
-                        xt[:].rearrange("p g u r -> p g r u"),
-                    )
+                turn_words(
+                    vraw[bc][:].bitcast(F32),
+                    lambda q: vgrp_w[:, 2 * q : 2 * q + 2, bc * P : (bc + 1) * P, :],
+                    (0, 2, 4, 6),
+                    4 * bc,
+                )
+            bt = ps_t.tile([P, P], BF16, name="bt", tag="xt")
+            nc.tensor.transpose(out=bt[:], in_=brow[:], identity=ident_b[:])
+            nc.vector.tensor_copy(out=bias[:], in_=bt[:, 0:32])
             for h in range(2):
                 nc.vector.quantize_mx(
                     out=vcodes[:, 1024 * h : 1024 * (h + 1)].bitcast(FP8X4),
@@ -120,59 +129,70 @@ def tile_hypernymvisual_acc_kernel(tc, vfs, p_lfs, n_lfs, W_hidden, b_hidden, W_
             ecodes = fix.tile([P, 4 * EMB], U32, align_bytes=64)
             escales = fix.tile([P, 4 * EMB], U8, align_bytes=64)
 
-            def side_work():
+            def side_turns():
                 for dc in range(4):
                     for gh in range(2):
-                        xb = ps_t.tile([P, 2, 4, P], BF16, tag="xt")
+                        xb = ps_t.tile([P, 2, 4, P], BF16, name="xb", tag="xt")
                         for gg in range(2):
                             for t in range(4):
                                 lo = dc * HID + 512 * (2 * gh + gg) + P * t
                                 nc.tensor.transpose(out=xb[:, gg, t, :], in_=weraw[:, lo : lo + P], identity=ident_b[:])
                         copy_out(
+                            gh == 1,
                             egrp_v[:, 2 * gh : 2 * gh + 2, dc * P : (dc + 1) * P, :],
                             xb[:].rearrange("p g t r -> p g r t"),
                         )
-                for h in range(2):
-                    nc.vector.quantize_mx(
-                        out=ecodes[:, 1024 * h : 1024 * (h + 1)].bitcast(FP8X4),
-                        scales=escales[:, 1024 * h : 1024 * (h + 1)],
-                        in_=egrp[:, 4096 * h : 4096 * (h + 1)],
-                    )
                 for ch in range(2):
-                    nb = ps_t.tile([P, 2, NNEG], BF16, tag="xt")
+                    nb = ps_t.tile([P, 2, NNEG], BF16, name="nb", tag="xt")
                     for cc in range(2):
                         for jc in range(4):
                             lo = jc * EMB + (2 * ch + cc) * P
                             nc.tensor.transpose(
                                 out=nb[:, cc, jc * P : (jc + 1) * P], in_=nraw[:, lo : lo + P], identity=ident_b[:]
                             )
-                    nc.vector.tensor_copy(out=nT[:, 2 * ch : 2 * ch + 2, :], in_=nb[:])
-                pb = ps_t.tile([P, 4, B], BF16, tag="xt")
+                    copy_out(ch == 1, nT[:, 2 * ch : 2 * ch + 2, :], nb[:])
+                pb = ps_t.tile([P, 4, B], BF16, name="pb", tag="xt")
                 for c in range(4):
                     for ic in range(2):
                         lo = ic * EMB + c * P
                         nc.tensor.transpose(
                             out=pb[:, c, ic * P : (ic + 1) * P], in_=praw[:, lo : lo + P], identity=ident_b[:]
                         )
-                nc.vector.tensor_copy(out=pT[:], in_=pb[:])
+                copy_out(False, pT[:], pb[:])
 
-            for hc in range(16):
-                if hc + 3 < 16:
-                    load_w(hc + 3)
-                words = wraws[hc][:].bitcast(F32)
-                wgrp = work.tile([P, VF], BF16, align_bytes=64)
+            def side_quantise():
+                for h in range(2):
+                    nc.vector.quantize_mx(
+                        out=ecodes[:, 1024 * h : 1024 * (h + 1)].bitcast(FP8X4),
+                        scales=escales[:, 1024 * h : 1024 * (h + 1)],
+                        in_=egrp[:, 4096 * h : 4096 * (h + 1)],
+                    )
+
+            wgrps = {}
+            wq = {}
+
+            def turn_w(hc):
+                wgrp = work.tile([P, VF], BF16, name="wgrp", tag="wgrp", bufs=3, align_bytes=64)
                 wgrp_w = wgrp[:].bitcast(F32).rearrange("p (g r u) -> p g r u", g=8, r=P, u=2)
-                for q in range(4):
-                    xt = ps_t.tile([P, 2, 2, P], F32, tag="xt")
-                    for gg in range(2):
-                        for u in range(2):
-                            lo = 256 * (2 * q + gg) + P * u
-                            nc.tensor.transpose(out=xt[:, gg, u, :], in_=words[:, lo : lo + P], identity=ident_f[:])
-                    copy_out(wgrp_w[:, 2 * q : 2 * q + 2, :, :], xt[:].rearrange("p g u r -> p g r u"))
-                wcodes = work.tile([P, 1024], U32, align_bytes=64)
-                wscales = work.tile([P, 1024], U8, align_bytes=64)
-                nc.vector.quantize_mx(out=wcodes[:].bitcast(FP8X4), scales=wscales[:], in_=wgrp[:])
-                acc = ps_a.tile([P, B], F32, tag="acc")
+                turn_words(
+                    wraws[hc][:].bitcast(F32),
+                    lambda q: wgrp_w[:, 2 * q : 2 * q + 2, :, :],
+                    ROUND_ON_VECTOR,
+                    4 * (hc % 2),
+                )
+                wgrps[hc] = wgrp
+                if hc + W_BUFS < 16:
+                    load_w(hc + W_BUFS)
+
+            def quantise_w(hc):
+                wcodes = work.tile([P, 1024], U32, name="wcodes", tag="wcodes", align_bytes=64)
+                wscales = work.tile([P, 1024], U8, name="wscales", tag="wscales", align_bytes=64)
+                nc.vector.quantize_mx(out=wcodes[:].bitcast(FP8X4), scales=wscales[:], in_=wgrps[hc][:])
+                wq[hc] = (wcodes, wscales)
+
+            def layer1(hc):
+                wcodes, wscales = wq[hc]
+                acc = ps_a.tile([P, B], F32, name="acc", tag="acc")
                 for g in range(8):
                     nc.tensor.matmul_mx(
                         out=acc[:],
@@ -183,21 +203,40 @@ def tile_hypernymvisual_acc_kernel(tc, vfs, p_lfs, n_lfs, W_hidden, b_hidden, W_
                         start=(g == 0),
                         stop=(g == 7),
                     )
-                g2, t = hc // 4, hc % 4
                 nc.scalar.activation(
-                    out=hgrp_v[:, g2, :, t], in_=acc[:], func=ACT.Identity, bias=bias[:, hc : hc + 1], scale=1.0
+                    out=hgrp_v[:, hc // 4, :, hc % 4], in_=acc[:], func=ACT.Identity, bias=bias[:, hc : hc + 1], scale=1.0
                 )
-                if t == 3:
-                    nc.vector.quantize_mx(
-                        out=hcodes[:, B * g2 : B * (g2 + 1)].bitcast(FP8X4),
-                        scales=hscales[:, B * g2 : B * (g2 + 1)],
-                        in_=hgrp[:, 4 * B * g2 : 4 * B * (g2 + 1)],
-                    )
-                if hc == 5:
-                    side_work()
+
+            def quantise_h(g2):
+                nc.vector.quantize_mx(
+                    out=hcodes[:, B * g2 : B * (g2 + 1)].bitcast(FP8X4),
+                    scales=hscales[:, B * g2 : B * (g2 + 1)],
+                    in_=hgrp[:, 4 * B * g2 : 4 * B * (g2 + 1)],
+                )
+
+            turn_w(0)
+            turn_w(1)
+            quantise_w(0)
+            quantise_w(1)
+            for rnd in range(1, 8):
+                if rnd == 3:
+                    side_turns()
+                turn_w(2 * rnd)
+                turn_w(2 * rnd + 1)
+                layer1(2 * rnd - 2)
+                layer1(2 * rnd - 1)
+                if rnd == 3:
+                    side_quantise()
+                quantise_w(2 * rnd)
+                quantise_w(2 * rnd + 1)
+                if rnd % 2 == 0:
+                    quantise_h(rnd // 2 - 1)
+            layer1(14)
+            layer1(15)
+            quantise_h(3)
 
             for dc in range(4):
-                acc = ps_a.tile([P, B], F32, tag="acc")
+                acc = ps_a.tile([P, B], F32, name="acc", tag="acc")
                 for g2 in range(4):
                     lo = EMB * g2 + P * dc
                     nc.tensor.matmul_mx(
@@ -209,33 +248,40 @@ def tile_hypernymvisual_acc_kernel(tc, vfs, p_lfs, n_lfs, W_hidden, b_hidden, W_
                         start=(g2 == 0),
                         stop=(g2 == 3),
                     )
-                nc.scalar.activation(
-                    out=eT[:, dc, :], in_=acc[:], func=ACT.Identity, bias=bias[:, 16 + dc : 17 + dc], scale=1.0
-                )
+                if dc % 2 == 0:
+                    nc.scalar.activation(
+                        out=eT[:, dc, :], in_=acc[:], func=ACT.Identity, bias=bias[:, 16 + dc : 17 + dc], scale=1.0
+                    )
+                else:
+                    nc.vector.tensor_scalar_add(out=eT[:, dc, :], in0=acc[:], scalar1=bias[:, 16 + dc : 17 + dc])
 
         fin = ctx.enter_context(tc.tile_pool(name="fin", bufs=1))
         rpool = ctx.enter_context(tc.tile_pool(name="rpool", bufs=R_BUFS))
         jpool = ctx.enter_context(tc.tile_pool(name="jpool", bufs=JUNK_BUFS))
         banks = ctx.enter_context(tc.psum_pool(name="banks", bufs=8))
 
-        acc_s = fin.tile([P, 3, B], F32)
-        stats = fin.tile([P, B, 6], F32)
+        stats = [fin.tile([P, P + N_EXTRA, 6], F32, name="stats%d" % ic) for ic in range(2)]
         acc_p = fin.tile([P, 2], F32)
+        rp = fin.tile([P, 4, B], F32)
 
         def square_sum(bank, dst):
             junk = jpool.tile([P, EMB], F32, name="junk", tag="junk")
             nc.scalar.activation(out=junk[:], in_=bank[:], func=ACT.Square, accum_out=dst)
 
-        rp = fin.tile([P, 4, B], F32)
-        nc.vector.tensor_tensor(out=rp[:], in0=pT[:], in1=eT[:], op=ALU.subtract)
-        nc.vector.tensor_scalar_max(out=rp[:], in0=rp[:], scalar1=0.0)
-        for ic in range(2):
-            bank = banks.tile([P, EMB], F32, name="bank", tag="bank")
+        def turn_into_bank(pieces):
+            bank = banks.tile([P, 4 * P], F32, name="bank", tag="bank")
             for c in range(4):
-                nc.tensor.transpose(
-                    out=bank[:, c * P : (c + 1) * P], in_=rp[:, c, ic * P : (ic + 1) * P], identity=ident_f[:]
-                )
-            square_sum(bank, acc_p[:, ic : ic + 1])
+                nc.tensor.transpose(out=bank[:, c * P : (c + 1) * P], in_=pieces[c], identity=ident_f[:])
+            return bank
+
+        def positives_diff():
+            nc.vector.tensor_tensor(out=rp[:], in0=pT[:], in1=eT[:], op=ALU.subtract)
+            nc.vector.tensor_scalar_max(out=rp[:], in0=rp[:], scalar1=0.0)
+
+        def positives_sum():
+            for ic in range(2):
+                bank = turn_into_bank([rp[:, c, ic * P : (ic + 1) * P] for c in range(4)])
+                square_sum(bank, acc_p[:, ic : ic + 1])
 
         r_tiles = {}
         bank_tiles = {}
@@ -256,43 +302,61 @@ def tile_hypernymvisual_acc_kernel(tc, vfs, p_lfs, n_lfs, W_hidden, b_hidden, W_
         def turn(i):
             r = r_tiles[i]
             for jc in range(4):
-                bank = banks.tile([P, EMB], F32, name="bank", tag="bank")
-                for c in range(4):
-                    nc.tensor.transpose(
-                        out=bank[:, c * P : (c + 1) * P], in_=r[:, c, jc * P : (jc + 1) * P], identity=ident_f[:]
-                    )
-                bank_tiles[(i, jc)] = bank
+                bank_tiles[(i, jc)] = turn_into_bank([r[:, c, jc * P : (jc + 1) * P] for c in range(4)])
 
         def reduce_row(i):
-            for jc in range(3):
+            extra = i % EXTRA_EVERY == EXTRA_AT
+            st = stats[i // P]
+            il = i % P
+            for jc in range(2 if extra else 3):
                 square_sum(bank_tiles[(i, jc)], acc_s[:, jc, i : i + 1])
-            nc.vector.bn_stats(out=stats[:, i, :], in_=bank_tiles[(i, 3)][:])
+            nc.vector.bn_stats(out=st[:, il, :], in_=bank_tiles[(i, 3)][:])
+            if extra:
+                nc.vector.bn_stats(out=st[:, P + il // EXTRA_EVERY, :], in_=bank_tiles[(i, 2)][:])
 
-        with tc.manual_schedule():
-            for s in range(B + 2):
-                if s < B:
-                    relu_diff(s)
-                if 0 <= s - 1 < B:
-                    turn(s - 1)
-                if 0 <= s - 2 < B:
-                    reduce_row(s - 2)
+        merged = {}
 
-        st = stats[:].rearrange("p i (h k) -> p i h k", h=2, k=3)
-        sq = fin.tile([P, B, 2], F32)
-        nc.vector.tensor_tensor(out=sq[:], in0=st[:, :, :, 1], in1=st[:, :, :, 1], op=ALU.mult)
-        nc.vector.scalar_tensor_tensor(
-            out=sq[:], in0=sq[:], scalar=float(EMB // 2), in1=st[:, :, :, 2], op0=ALU.mult, op1=ALU.add
-        )
-        acc_v = fin.tile([P, B], F32)
-        nc.vector.tensor_tensor(out=acc_v[:], in0=sq[:, :, 0], in1=sq[:, :, 1], op=ALU.add)
+        def finish_sums(ic):
+            rows = slice(ic * P, (ic + 1) * P)
+            st = stats[ic][:].rearrange("p s (h k) -> p s h k", h=2, k=3)
+            sq = fin.tile([P, P + N_EXTRA, 2], F32, name="sq%d" % ic)
+            nc.vector.tensor_tensor(out=sq[:], in0=st[:, :, :, 1], in1=st[:, :, :, 1], op=ALU.mult)
+            nc.vector.scalar_tensor_tensor(
+                out=sq[:], in0=sq[:], scalar=float(EMB // 2), in1=st[:, :, :, 2], op0=ALU.mult, op1=ALU.add
+            )
+            sv = fin.tile([P, P + N_EXTRA], F32, name="sv%d" % ic)
+            nc.vector.tensor_tensor(out=sv[:], in0=sq[:, :, 0], in1=sq[:, :, 1], op=ALU.add)
+            mixed = fin.tile([P, P], F32, name="mixed%d" % ic)
+            nc.vector.tensor_copy(out=mixed[:], in_=acc_s[:, 2, rows])
+            nc.vector.tensor_copy(
+                out=mixed[:].rearrange("p (a b) -> p a b", b=EXTRA_EVERY)[:, :, EXTRA_AT], in_=sv[:, P : P + N_EXTRA]
+            )
+            merged[ic] = (mixed, sv)
 
-        for ic in range(2):
-            bank = banks.tile([P, NNEG], F32, name="bank", tag="bank")
-            for jc in range(4):
-                src = acc_s[:, jc, ic * P : (ic + 1) * P] if jc < 3 else acc_v[:, ic * P : (ic + 1) * P]
-                nc.tensor.transpose(out=bank[:, jc * P : (jc + 1) * P], in_=src, identity=ident_f[:])
+        def finish_store(ic):
+            rows = slice(ic * P, (ic + 1) * P)
+            mixed, sv = merged[ic]
+            bank = turn_into_bank([acc_s[:, 0, rows], acc_s[:, 1, rows], mixed[:], sv[:, 0:P]])
             res = fin.tile([P, NNEG + 1], F32, name="res%d" % ic)
             nc.scalar.activation(out=res[:, 0:1], in_=acc_p[:, ic : ic + 1], func=ACT.Sqrt)
             nc.scalar.activation(out=res[:, 1 : NNEG + 1], in_=bank[:], func=ACT.Sqrt)
             nc.vector.tensor_scalar_mul(out=res[:], in0=res[:], scalar1=-1.0)
-            nc.sync.dma_start(out=out[ic * P : (ic + 1) * P, :], in_=res[:])
+            nc.sync.dma_start(out=out[rows, :], in_=res[:])
+
+        for s in range(B + 2):
+            if s < B:
+                relu_diff(s)
+            if 0 <= s - 1 < B:
+                turn(s - 1)
+            if 0 <= s - 2 < B:
+                reduce_row(s - 2)
+            if s == 6:
+                positives_diff()
+            if s == 8:
+                positives_sum()
+            if s == P + 6:
+                finish_sums(0)
+            if s == P + 8:
+                finish_store(0)
+        finish_sums(1)
+        finish_store(1)

@@ -18,10 +18,11 @@ FLOPS = 2 * B * VF * HID + 2 * B * HID * EMB + 4 * B * (NNEG + 1) * EMB
 W_BUFS = 6
 R_BUFS = 4
 JUNK_BUFS = 4
-EXTRA_EVERY = 8
-EXTRA_AT = 3
-N_EXTRA = P // EXTRA_EVERY
 ROUND_ON_VECTOR = (3, 6, 7)
+
+
+def on_vector(i, jc):
+    return jc == 3
 
 
 def tile_hypernymvisual_acc_kernel(tc, vfs, p_lfs, n_lfs, W_hidden, b_hidden, W_embed, b_embed, out):
@@ -37,8 +38,11 @@ def tile_hypernymvisual_acc_kernel(tc, vfs, p_lfs, n_lfs, W_hidden, b_hidden, W_
         pT = keep.tile([P, 4, B], F32)
         eT = keep.tile([P, 4, B], F32)
         bias = keep.tile([P, 32], F32)
-        acc_s = keep.tile([P, 3, B], F32)
+        acc_s = keep.tile([P, 4, B], F32)
         nc.gpsimd.memset(acc_s[:], 0.0)
+        stats = [keep.tile([P, 2, P, 6], F32, name="stats%d" % ic) for ic in range(2)]
+        for ic in range(2):
+            nc.gpsimd.memset(stats[ic][:], 0.0)
         one = keep.tile([P, 1], F32)
         nc.vector.memset(one[:], 1.0)
         warm = keep.tile([P, 1], F32)
@@ -260,7 +264,6 @@ def tile_hypernymvisual_acc_kernel(tc, vfs, p_lfs, n_lfs, W_hidden, b_hidden, W_
         jpool = ctx.enter_context(tc.tile_pool(name="jpool", bufs=JUNK_BUFS))
         banks = ctx.enter_context(tc.psum_pool(name="banks", bufs=8))
 
-        stats = [fin.tile([P, P + N_EXTRA, 6], F32, name="stats%d" % ic) for ic in range(2)]
         acc_p = fin.tile([P, 2], F32)
         rp = fin.tile([P, 4, B], F32)
 
@@ -305,38 +308,34 @@ def tile_hypernymvisual_acc_kernel(tc, vfs, p_lfs, n_lfs, W_hidden, b_hidden, W_
                 bank_tiles[(i, jc)] = turn_into_bank([r[:, c, jc * P : (jc + 1) * P] for c in range(4)])
 
         def reduce_row(i):
-            extra = i % EXTRA_EVERY == EXTRA_AT
-            st = stats[i // P]
-            il = i % P
-            for jc in range(2 if extra else 3):
-                square_sum(bank_tiles[(i, jc)], acc_s[:, jc, i : i + 1])
-            nc.vector.bn_stats(out=st[:, il, :], in_=bank_tiles[(i, 3)][:])
-            if extra:
-                nc.vector.bn_stats(out=st[:, P + il // EXTRA_EVERY, :], in_=bank_tiles[(i, 2)][:])
+            for jc in range(4):
+                if not on_vector(i, jc):
+                    square_sum(bank_tiles[(i, jc)], acc_s[:, jc, i : i + 1])
+            for jc in range(2, 4):
+                if on_vector(i, jc):
+                    nc.vector.bn_stats(out=stats[i // P][:, jc - 2, i % P, :], in_=bank_tiles[(i, jc)][:])
 
         merged = {}
 
         def finish_sums(ic):
             rows = slice(ic * P, (ic + 1) * P)
-            st = stats[ic][:].rearrange("p s (h k) -> p s h k", h=2, k=3)
-            sq = fin.tile([P, P + N_EXTRA, 2], F32, name="sq%d" % ic)
+            st = stats[ic][:].rearrange("p a s (h k) -> p (a s) h k", h=2, k=3)
+            sq = fin.tile([P, 2 * P, 2], F32, name="sq%d" % ic)
             nc.vector.tensor_tensor(out=sq[:], in0=st[:, :, :, 1], in1=st[:, :, :, 1], op=ALU.mult)
             nc.vector.scalar_tensor_tensor(
                 out=sq[:], in0=sq[:], scalar=float(EMB // 2), in1=st[:, :, :, 2], op0=ALU.mult, op1=ALU.add
             )
-            sv = fin.tile([P, P + N_EXTRA], F32, name="sv%d" % ic)
-            nc.vector.tensor_tensor(out=sv[:], in0=sq[:, :, 0], in1=sq[:, :, 1], op=ALU.add)
-            mixed = fin.tile([P, P], F32, name="mixed%d" % ic)
-            nc.vector.tensor_copy(out=mixed[:], in_=acc_s[:, 2, rows])
-            nc.vector.tensor_copy(
-                out=mixed[:].rearrange("p (a b) -> p a b", b=EXTRA_EVERY)[:, :, EXTRA_AT], in_=sv[:, P : P + N_EXTRA]
+            sv = fin.tile([P, 2, P], F32, name="sv%d" % ic)
+            nc.vector.tensor_tensor(
+                out=sv[:].rearrange("p a s -> p (a s)"), in0=sq[:, :, 0], in1=sq[:, :, 1], op=ALU.add
             )
-            merged[ic] = (mixed, sv)
+            nc.vector.tensor_tensor(out=sv[:], in0=sv[:], in1=acc_s[:, 2:4, rows], op=ALU.add)
+            merged[ic] = sv
 
         def finish_store(ic):
             rows = slice(ic * P, (ic + 1) * P)
-            mixed, sv = merged[ic]
-            bank = turn_into_bank([acc_s[:, 0, rows], acc_s[:, 1, rows], mixed[:], sv[:, 0:P]])
+            sv = merged[ic]
+            bank = turn_into_bank([acc_s[:, 0, rows], acc_s[:, 1, rows], sv[:, 0, :], sv[:, 1, :]])
             res = fin.tile([P, NNEG + 1], F32, name="res%d" % ic)
             nc.scalar.activation(out=res[:, 0:1], in_=acc_p[:, ic : ic + 1], func=ACT.Sqrt)
             nc.scalar.activation(out=res[:, 1 : NNEG + 1], in_=bank[:], func=ACT.Sqrt)

@@ -16,13 +16,16 @@ B, NNEG, VF, HID, EMB = 256, 512, 4096, 2048, 512
 FLOPS = 2 * B * VF * HID + 2 * B * HID * EMB + 4 * B * (NNEG + 1) * EMB
 
 W_BUFS = 6
-R_BUFS = 4
+R_BUFS = 7
+G_AHEAD = 3
+G_CHUNK = 3
+BIG = 3.0e38
 JUNK_BUFS = 4
 ROUND_ON_VECTOR = (3, 6, 7)
 
 
 def on_vector(i, jc):
-    return jc == 3
+    return jc == 3 or (jc == 2 and (i * 9) % 32 < 9)
 
 
 def tile_hypernymvisual_acc_kernel(tc, vfs, p_lfs, n_lfs, W_hidden, b_hidden, W_embed, b_embed, out):
@@ -271,11 +274,32 @@ def tile_hypernymvisual_acc_kernel(tc, vfs, p_lfs, n_lfs, W_hidden, b_hidden, W_
             junk = jpool.tile([P, EMB], F32, name="junk", tag="junk")
             nc.scalar.activation(out=junk[:], in_=bank[:], func=ACT.Square, accum_out=dst)
 
-        def turn_into_bank(pieces):
+        def turn_into_bank(pieces, shift=None):
             bank = banks.tile([P, 4 * P], F32, name="bank", tag="bank")
             for c in range(4):
-                nc.tensor.transpose(out=bank[:, c * P : (c + 1) * P], in_=pieces[c], identity=ident_f[:])
+                if shift is not None and c == G_CHUNK:
+                    nc.tensor.matmul(
+                        out=bank[:, c * P : (c + 1) * P],
+                        lhsT=pieces[c],
+                        rhs=ident_f[:],
+                        is_transpose=True,
+                        start=True,
+                        stop=False,
+                    )
+                    nc.tensor.matmul(
+                        out=bank[:, c * P : (c + 1) * P],
+                        lhsT=shift.to_broadcast([P, P]),
+                        rhs=ident_f[:],
+                        is_transpose=True,
+                        start=False,
+                        stop=True,
+                    )
+                else:
+                    nc.tensor.transpose(out=bank[:, c * P : (c + 1) * P], in_=pieces[c], identity=ident_f[:])
             return bank
+
+        neg_e = fin.tile([P, B], F32)
+        nc.vector.tensor_scalar_mul(out=neg_e[:], in0=eT[:, G_CHUNK, :], scalar1=-1.0)
 
         def positives_diff():
             nc.vector.tensor_tensor(out=rp[:], in0=pT[:], in1=eT[:], op=ALU.subtract)
@@ -289,9 +313,21 @@ def tile_hypernymvisual_acc_kernel(tc, vfs, p_lfs, n_lfs, W_hidden, b_hidden, W_
         r_tiles = {}
         bank_tiles = {}
 
-        def relu_diff(i):
+        def clamp_low(i):
             r = rpool.tile([P, 4, NNEG], F32, name="r", tag="r")
-            for c in range(4):
+            nc.gpsimd.tensor_scalar(
+                out=r[:, G_CHUNK, :],
+                in0=nT[:, G_CHUNK, :],
+                scalar1=BIG,
+                scalar2=eT[:, G_CHUNK, i : i + 1],
+                op0=ALU.min,
+                op1=ALU.max,
+            )
+            r_tiles[i] = r
+
+        def relu_diff(i):
+            r = r_tiles[i]
+            for c in range(3):
                 nc.vector.tensor_scalar(
                     out=r[:, c, :],
                     in0=nT[:, c, :],
@@ -300,12 +336,13 @@ def tile_hypernymvisual_acc_kernel(tc, vfs, p_lfs, n_lfs, W_hidden, b_hidden, W_
                     op0=ALU.subtract,
                     op1=ALU.max,
                 )
-            r_tiles[i] = r
 
         def turn(i):
             r = r_tiles[i]
             for jc in range(4):
-                bank_tiles[(i, jc)] = turn_into_bank([r[:, c, jc * P : (jc + 1) * P] for c in range(4)])
+                bank_tiles[(i, jc)] = turn_into_bank(
+                    [r[:, c, jc * P : (jc + 1) * P] for c in range(4)], neg_e[:, i : i + 1]
+                )
 
         def reduce_row(i):
             for jc in range(4):
@@ -342,7 +379,11 @@ def tile_hypernymvisual_acc_kernel(tc, vfs, p_lfs, n_lfs, W_hidden, b_hidden, W_
             nc.vector.tensor_scalar_mul(out=res[:], in0=res[:], scalar1=-1.0)
             nc.sync.dma_start(out=out[rows, :], in_=res[:])
 
+        for i in range(G_AHEAD):
+            clamp_low(i)
         for s in range(B + 2):
+            if s + G_AHEAD < B:
+                clamp_low(s + G_AHEAD)
             if s < B:
                 relu_diff(s)
             if 0 <= s - 1 < B:

@@ -16,16 +16,11 @@ B, NNEG, VF, HID, EMB = 256, 512, 4096, 2048, 512
 FLOPS = 2 * B * VF * HID + 2 * B * HID * EMB + 4 * B * (NNEG + 1) * EMB
 
 W_BUFS = 6
-R_BUFS = 7
-G_AHEAD = 3
-G_CHUNK = 3
-BIG = 3.0e38
+R_BUFS = 4
 JUNK_BUFS = 4
 ROUND_ON_VECTOR = (3, 6, 7)
 
-
-def on_vector(i, jc):
-    return jc == 3 or (jc == 2 and (i * 9) % 32 < 9)
+LATE_ROWS = 8
 
 
 def tile_hypernymvisual_acc_kernel(tc, vfs, p_lfs, n_lfs, W_hidden, b_hidden, W_embed, b_embed, out):
@@ -41,11 +36,8 @@ def tile_hypernymvisual_acc_kernel(tc, vfs, p_lfs, n_lfs, W_hidden, b_hidden, W_
         pT = keep.tile([P, 4, B], F32)
         eT = keep.tile([P, 4, B], F32)
         bias = keep.tile([P, 32], F32)
-        acc_s = keep.tile([P, 4, B], F32)
-        nc.gpsimd.memset(acc_s[:], 0.0)
-        stats = [keep.tile([P, 2, P, 6], F32, name="stats%d" % ic) for ic in range(2)]
-        for ic in range(2):
-            nc.gpsimd.memset(stats[ic][:], 0.0)
+        acc_s = keep.tile([P, 3, B], F32)
+        stats = keep.tile([P, B + 2, 6], F32)
         one = keep.tile([P, 1], F32)
         nc.vector.memset(one[:], 1.0)
         warm = keep.tile([P, 1], F32)
@@ -222,21 +214,24 @@ def tile_hypernymvisual_acc_kernel(tc, vfs, p_lfs, n_lfs, W_hidden, b_hidden, W_
                 )
 
             turn_w(0)
-            turn_w(1)
             quantise_w(0)
-            quantise_w(1)
-            for rnd in range(1, 8):
-                if rnd == 3:
-                    side_turns()
+            for hc in range(1, 4):
+                turn_w(hc)
+                layer1(hc - 1)
+                quantise_w(hc)
+            side_turns()
+            layer1(3)
+            side_quantise()
+            quantise_h(0)
+            for rnd in range(2, 8):
                 turn_w(2 * rnd)
                 turn_w(2 * rnd + 1)
-                layer1(2 * rnd - 2)
-                layer1(2 * rnd - 1)
-                if rnd == 3:
-                    side_quantise()
+                if rnd > 2:
+                    layer1(2 * rnd - 2)
+                    layer1(2 * rnd - 1)
                 quantise_w(2 * rnd)
                 quantise_w(2 * rnd + 1)
-                if rnd % 2 == 0:
+                if rnd > 2 and rnd % 2 == 0:
                     quantise_h(rnd // 2 - 1)
             layer1(14)
             layer1(15)
@@ -267,39 +262,19 @@ def tile_hypernymvisual_acc_kernel(tc, vfs, p_lfs, n_lfs, W_hidden, b_hidden, W_
         jpool = ctx.enter_context(tc.tile_pool(name="jpool", bufs=JUNK_BUFS))
         banks = ctx.enter_context(tc.psum_pool(name="banks", bufs=8))
 
-        acc_p = fin.tile([P, 2], F32)
         rp = fin.tile([P, 4, B], F32)
+        sq = fin.tile([P, B + 2, 2], F32)
+        sums = fin.tile([P, B + 2], F32)
 
         def square_sum(bank, dst):
             junk = jpool.tile([P, EMB], F32, name="junk", tag="junk")
             nc.scalar.activation(out=junk[:], in_=bank[:], func=ACT.Square, accum_out=dst)
 
-        def turn_into_bank(pieces, shift=None):
+        def turn_into_bank(pieces):
             bank = banks.tile([P, 4 * P], F32, name="bank", tag="bank")
             for c in range(4):
-                if shift is not None and c == G_CHUNK:
-                    nc.tensor.matmul(
-                        out=bank[:, c * P : (c + 1) * P],
-                        lhsT=pieces[c],
-                        rhs=ident_f[:],
-                        is_transpose=True,
-                        start=True,
-                        stop=False,
-                    )
-                    nc.tensor.matmul(
-                        out=bank[:, c * P : (c + 1) * P],
-                        lhsT=shift.to_broadcast([P, P]),
-                        rhs=ident_f[:],
-                        is_transpose=True,
-                        start=False,
-                        stop=True,
-                    )
-                else:
-                    nc.tensor.transpose(out=bank[:, c * P : (c + 1) * P], in_=pieces[c], identity=ident_f[:])
+                nc.tensor.transpose(out=bank[:, c * P : (c + 1) * P], in_=pieces[c], identity=ident_f[:])
             return bank
-
-        neg_e = fin.tile([P, B], F32)
-        nc.vector.tensor_scalar_mul(out=neg_e[:], in0=eT[:, G_CHUNK, :], scalar1=-1.0)
 
         def positives_diff():
             nc.vector.tensor_tensor(out=rp[:], in0=pT[:], in1=eT[:], op=ALU.subtract)
@@ -308,26 +283,14 @@ def tile_hypernymvisual_acc_kernel(tc, vfs, p_lfs, n_lfs, W_hidden, b_hidden, W_
         def positives_sum():
             for ic in range(2):
                 bank = turn_into_bank([rp[:, c, ic * P : (ic + 1) * P] for c in range(4)])
-                square_sum(bank, acc_p[:, ic : ic + 1])
+                nc.vector.bn_stats(out=stats[:, B + ic, :], in_=bank[:])
 
         r_tiles = {}
         bank_tiles = {}
 
-        def clamp_low(i):
-            r = rpool.tile([P, 4, NNEG], F32, name="r", tag="r")
-            nc.gpsimd.tensor_scalar(
-                out=r[:, G_CHUNK, :],
-                in0=nT[:, G_CHUNK, :],
-                scalar1=BIG,
-                scalar2=eT[:, G_CHUNK, i : i + 1],
-                op0=ALU.min,
-                op1=ALU.max,
-            )
-            r_tiles[i] = r
-
         def relu_diff(i):
-            r = r_tiles[i]
-            for c in range(3):
+            r = rpool.tile([P, 4, NNEG], F32, name="r", tag="r")
+            for c in range(4):
                 nc.vector.tensor_scalar(
                     out=r[:, c, :],
                     in0=nT[:, c, :],
@@ -336,54 +299,41 @@ def tile_hypernymvisual_acc_kernel(tc, vfs, p_lfs, n_lfs, W_hidden, b_hidden, W_
                     op0=ALU.subtract,
                     op1=ALU.max,
                 )
+            r_tiles[i] = r
 
         def turn(i):
             r = r_tiles[i]
             for jc in range(4):
-                bank_tiles[(i, jc)] = turn_into_bank(
-                    [r[:, c, jc * P : (jc + 1) * P] for c in range(4)], neg_e[:, i : i + 1]
-                )
+                bank_tiles[(i, jc)] = turn_into_bank([r[:, c, jc * P : (jc + 1) * P] for c in range(4)])
 
         def reduce_row(i):
-            for jc in range(4):
-                if not on_vector(i, jc):
-                    square_sum(bank_tiles[(i, jc)], acc_s[:, jc, i : i + 1])
-            for jc in range(2, 4):
-                if on_vector(i, jc):
-                    nc.vector.bn_stats(out=stats[i // P][:, jc - 2, i % P, :], in_=bank_tiles[(i, jc)][:])
+            for jc in range(3):
+                square_sum(bank_tiles[(i, jc)], acc_s[:, jc, i : i + 1])
+            nc.vector.bn_stats(out=stats[:, i, :], in_=bank_tiles[(i, 3)][:])
 
-        merged = {}
-
-        def finish_sums(ic):
-            rows = slice(ic * P, (ic + 1) * P)
-            st = stats[ic][:].rearrange("p a s (h k) -> p (a s) h k", h=2, k=3)
-            sq = fin.tile([P, 2 * P, 2], F32, name="sq%d" % ic)
-            nc.vector.tensor_tensor(out=sq[:], in0=st[:, :, :, 1], in1=st[:, :, :, 1], op=ALU.mult)
+        def sums_from_stats(lo, hi):
+            st = stats[:, lo:hi, :].rearrange("p s (h k) -> p s h k", h=2, k=3)
+            nc.vector.tensor_tensor(out=sq[:, lo:hi, :], in0=st[:, :, :, 1], in1=st[:, :, :, 1], op=ALU.mult)
             nc.vector.scalar_tensor_tensor(
-                out=sq[:], in0=sq[:], scalar=float(EMB // 2), in1=st[:, :, :, 2], op0=ALU.mult, op1=ALU.add
+                out=sq[:, lo:hi, :],
+                in0=sq[:, lo:hi, :],
+                scalar=float(EMB // 2),
+                in1=st[:, :, :, 2],
+                op0=ALU.mult,
+                op1=ALU.add,
             )
-            sv = fin.tile([P, 2, P], F32, name="sv%d" % ic)
-            nc.vector.tensor_tensor(
-                out=sv[:].rearrange("p a s -> p (a s)"), in0=sq[:, :, 0], in1=sq[:, :, 1], op=ALU.add
-            )
-            nc.vector.tensor_tensor(out=sv[:], in0=sv[:], in1=acc_s[:, 2:4, rows], op=ALU.add)
-            merged[ic] = sv
+            nc.vector.tensor_tensor(out=sums[:, lo:hi], in0=sq[:, lo:hi, 0], in1=sq[:, lo:hi, 1], op=ALU.add)
 
         def finish_store(ic):
             rows = slice(ic * P, (ic + 1) * P)
-            sv = merged[ic]
-            bank = turn_into_bank([acc_s[:, 0, rows], acc_s[:, 1, rows], sv[:, 0, :], sv[:, 1, :]])
+            bank = turn_into_bank([acc_s[:, 0, rows], acc_s[:, 1, rows], acc_s[:, 2, rows], sums[:, rows]])
             res = fin.tile([P, NNEG + 1], F32, name="res%d" % ic)
-            nc.scalar.activation(out=res[:, 0:1], in_=acc_p[:, ic : ic + 1], func=ACT.Sqrt)
+            nc.scalar.activation(out=res[:, 0:1], in_=sums[:, B + ic : B + ic + 1], func=ACT.Sqrt)
             nc.scalar.activation(out=res[:, 1 : NNEG + 1], in_=bank[:], func=ACT.Sqrt)
             nc.vector.tensor_scalar_mul(out=res[:], in0=res[:], scalar1=-1.0)
             nc.sync.dma_start(out=out[rows, :], in_=res[:])
 
-        for i in range(G_AHEAD):
-            clamp_low(i)
         for s in range(B + 2):
-            if s + G_AHEAD < B:
-                clamp_low(s + G_AHEAD)
             if s < B:
                 relu_diff(s)
             if 0 <= s - 1 < B:
@@ -394,9 +344,13 @@ def tile_hypernymvisual_acc_kernel(tc, vfs, p_lfs, n_lfs, W_hidden, b_hidden, W_
                 positives_diff()
             if s == 8:
                 positives_sum()
+            if s == 12:
+                sums_from_stats(B, B + 2)
             if s == P + 6:
-                finish_sums(0)
+                sums_from_stats(0, P)
             if s == P + 8:
                 finish_store(0)
-        finish_sums(1)
+            if s == B - LATE_ROWS + 4:
+                sums_from_stats(P, B - LATE_ROWS)
+        sums_from_stats(B - LATE_ROWS, B)
         finish_store(1)

@@ -16,11 +16,8 @@ B, NNEG, VF, HID, EMB = 256, 512, 4096, 2048, 512
 FLOPS = 2 * B * VF * HID + 2 * B * HID * EMB + 4 * B * (NNEG + 1) * EMB
 
 W_BUFS = 6
-R_BUFS = 4
-JUNK_BUFS = 4
+M_BUFS = 4
 ROUND_ON_VECTOR = (3, 6, 7)
-
-LATE_ROWS = 8
 
 
 def tile_hypernymvisual_acc_kernel(tc, vfs, p_lfs, n_lfs, W_hidden, b_hidden, W_embed, b_embed, out):
@@ -32,12 +29,12 @@ def tile_hypernymvisual_acc_kernel(tc, vfs, p_lfs, n_lfs, W_hidden, b_hidden, W_
         make_identity(nc, ident_f[:])
         ident_b = keep.tile([P, P], BF16)
         make_identity(nc, ident_b[:])
-        nT = keep.tile([P, 4, NNEG], F32)
+        nT = keep.tile([P, 4, NNEG], BF16)
         pT = keep.tile([P, 4, B], F32)
         eT = keep.tile([P, 4, B], F32)
+        ehT = keep.tile([P, 4, B], BF16)
+        nraw = keep.tile([P, 4 * EMB], BF16)
         bias = keep.tile([P, 32], F32)
-        acc_s = keep.tile([P, 3, B], F32)
-        stats = keep.tile([P, B + 2, 6], F32)
         one = keep.tile([P, 1], F32)
         nc.vector.memset(one[:], 1.0)
         warm = keep.tile([P, 1], F32)
@@ -66,7 +63,6 @@ def tile_hypernymvisual_acc_kernel(tc, vfs, p_lfs, n_lfs, W_hidden, b_hidden, W_
                 nc.sync.dma_start(out=t[:], in_=vfs[bc * P : (bc + 1) * P, :])
                 vraw.append(t)
             weraw = fix.tile([P, 4 * HID], BF16)
-            nraw = fix.tile([P, 4 * EMB], BF16)
             praw = fix.tile([P, 2 * EMB], BF16)
             wraws = []
 
@@ -250,31 +246,99 @@ def tile_hypernymvisual_acc_kernel(tc, vfs, p_lfs, n_lfs, W_hidden, b_hidden, W_
                         start=(g2 == 0),
                         stop=(g2 == 3),
                     )
-                if dc % 2 == 0:
-                    nc.scalar.activation(
-                        out=eT[:, dc, :], in_=acc[:], func=ACT.Identity, bias=bias[:, 16 + dc : 17 + dc], scale=1.0
-                    )
-                else:
-                    nc.vector.tensor_scalar_add(out=eT[:, dc, :], in0=acc[:], scalar1=bias[:, 16 + dc : 17 + dc])
+                nc.scalar.activation(
+                    out=eT[:, dc, :], in_=acc[:], func=ACT.Identity, bias=bias[:, 16 + dc : 17 + dc], scale=1.0
+                )
+                nc.vector.tensor_copy(out=ehT[:, dc, :], in_=eT[:, dc, :])
 
         fin = ctx.enter_context(tc.tile_pool(name="fin", bufs=1))
-        rpool = ctx.enter_context(tc.tile_pool(name="rpool", bufs=R_BUFS))
-        jpool = ctx.enter_context(tc.tile_pool(name="jpool", bufs=JUNK_BUFS))
-        banks = ctx.enter_context(tc.psum_pool(name="banks", bufs=8))
+        mpool = ctx.enter_context(tc.tile_pool(name="mpool", bufs=M_BUFS))
+        banks = ctx.enter_context(tc.psum_pool(name="banks", bufs=2))
 
+        ones = fin.tile([P, 2], F32)
+        nc.vector.memset(ones[:], 1.0)
+        el = fin.tile([P, 4, B], F32)
+        w2 = fin.tile([P, 4, B, 2], BF16)
+        kk = fin.tile([P, 4, B], F32)
+        ki = fin.tile([P, 2], F32)
         rp = fin.tile([P, 4, B], F32)
-        sq = fin.tile([P, B + 2, 2], F32)
-        sums = fin.tile([P, B + 2], F32)
+        nn = fin.tile([P, 4], F32)
+        psum_sq = fin.tile([P, 2], F32)
+        qs = fin.tile([P, 2, NNEG], F32)
+        tj = fin.tile([P, 4, B], F32)
+        uj = fin.tile([P, 4, B], F32)
 
-        def square_sum(bank, dst):
-            junk = jpool.tile([P, EMB], F32, name="junk", tag="junk")
-            nc.scalar.activation(out=junk[:], in_=bank[:], func=ACT.Square, accum_out=dst)
+        for jc in range(4):
+            junk = mpool.tile([P, EMB], F32, name="junk", tag="junk")
+            nc.scalar.activation(
+                out=junk[:], in_=nraw[:, jc * EMB : (jc + 1) * EMB], func=ACT.Square, accum_out=nn[:, jc : jc + 1]
+            )
 
         def turn_into_bank(pieces):
             bank = banks.tile([P, 4 * P], F32, name="bank", tag="bank")
             for c in range(4):
                 nc.tensor.transpose(out=bank[:, c * P : (c + 1) * P], in_=pieces[c], identity=ident_f[:])
             return bank
+
+        q_tiles = {}
+
+        def min_row(j):
+            q = mpool.tile([P, 4, B], BF16, name="q", tag="q")
+            for c in range(4):
+                nc.vector.tensor_scalar_min(out=q[:, c, :], in0=ehT[:, c, :], scalar1=nT[:, c, j : j + 1])
+            q_tiles[j] = q
+
+        def sum_min(j, qbank, col):
+            for ic in range(2):
+                for c in range(4):
+                    nc.tensor.matmul(
+                        out=qbank[:, ic, col : col + 1],
+                        lhsT=q_tiles[j][:, c, ic * P : (ic + 1) * P],
+                        rhs=nT[:, c, j : j + 1],
+                        start=(c == 0),
+                        stop=(c == 3),
+                    )
+
+        m_tiles = {}
+
+        def max_row(i):
+            m = mpool.tile([P, 4, NNEG], BF16, name="m", tag="m")
+            for c in range(4):
+                nc.vector.tensor_scalar_max(out=m[:, c, :], in0=nT[:, c, :], scalar1=ehT[:, c, i : i + 1])
+            m_tiles[i] = m
+
+        def sum_max(i, abank, col):
+            for jc in range(4):
+                for c in range(4):
+                    nc.tensor.matmul(
+                        out=abank[:, jc, col, :],
+                        lhsT=m_tiles[i][:, c, jc * P : (jc + 1) * P],
+                        rhs=w2[:, c, i, :],
+                        start=(c == 0),
+                        stop=(c == 3),
+                    )
+
+        def split_e():
+            nc.vector.tensor_tensor(out=el[:], in0=eT[:], in1=ehT[:], op=ALU.subtract)
+            nc.scalar.copy(out=w2[:, :, :, 0], in_=ehT[:])
+            nc.scalar.mul(out=w2[:, :, :, 1], in_=el[:], mul=2.0)
+
+        def row_constants():
+            nc.vector.tensor_tensor(out=kk[:], in0=w2[:, :, :, 0], in1=w2[:, :, :, 1], op=ALU.add)
+            nc.vector.tensor_tensor(out=kk[:], in0=kk[:], in1=ehT[:], op=ALU.mult)
+
+        def row_constants_sum():
+            kbank = banks.tile([P, 2, 2], F32, name="kbank", tag="bank")
+            for ic in range(2):
+                for c in range(4):
+                    nc.tensor.matmul(
+                        out=kbank[:, ic, :],
+                        lhsT=kk[:, c, ic * P : (ic + 1) * P],
+                        rhs=ones[:],
+                        start=(c == 0),
+                        stop=(c == 3),
+                    )
+            nc.vector.tensor_copy(out=ki[:], in_=kbank[:, :, 0])
 
         def positives_diff():
             nc.vector.tensor_tensor(out=rp[:], in0=pT[:], in1=eT[:], op=ALU.subtract)
@@ -283,74 +347,55 @@ def tile_hypernymvisual_acc_kernel(tc, vfs, p_lfs, n_lfs, W_hidden, b_hidden, W_
         def positives_sum():
             for ic in range(2):
                 bank = turn_into_bank([rp[:, c, ic * P : (ic + 1) * P] for c in range(4)])
-                nc.vector.bn_stats(out=stats[:, B + ic, :], in_=bank[:])
+                junk = mpool.tile([P, EMB], F32, name="junk", tag="junk")
+                nc.scalar.activation(out=junk[:], in_=bank[:], func=ACT.Square, accum_out=psum_sq[:, ic : ic + 1])
 
-        r_tiles = {}
-        bank_tiles = {}
-
-        def relu_diff(i):
-            r = rpool.tile([P, 4, NNEG], F32, name="r", tag="r")
-            for c in range(4):
-                nc.vector.tensor_scalar(
-                    out=r[:, c, :],
-                    in0=nT[:, c, :],
-                    scalar1=eT[:, c, i : i + 1],
-                    scalar2=0.0,
-                    op0=ALU.subtract,
-                    op1=ALU.max,
-                )
-            r_tiles[i] = r
-
-        def turn(i):
-            r = r_tiles[i]
-            for jc in range(4):
-                bank_tiles[(i, jc)] = turn_into_bank([r[:, c, jc * P : (jc + 1) * P] for c in range(4)])
-
-        def reduce_row(i):
-            for jc in range(3):
-                square_sum(bank_tiles[(i, jc)], acc_s[:, jc, i : i + 1])
-            nc.vector.bn_stats(out=stats[:, i, :], in_=bank_tiles[(i, 3)][:])
-
-        def sums_from_stats(lo, hi):
-            st = stats[:, lo:hi, :].rearrange("p s (h k) -> p s h k", h=2, k=3)
-            nc.vector.tensor_tensor(out=sq[:, lo:hi, :], in0=st[:, :, :, 1], in1=st[:, :, :, 1], op=ALU.mult)
-            nc.vector.scalar_tensor_tensor(
-                out=sq[:, lo:hi, :],
-                in0=sq[:, lo:hi, :],
-                scalar=float(EMB // 2),
-                in1=st[:, :, :, 2],
-                op0=ALU.mult,
-                op1=ALU.add,
-            )
-            nc.vector.tensor_tensor(out=sums[:, lo:hi], in0=sq[:, lo:hi, 0], in1=sq[:, lo:hi, 1], op=ALU.add)
+        for h in range(2):
+            qbank = banks.tile([P, 2, 256], F32, name="qbank", tag="qbank")
+            for s in range(257):
+                j = 256 * h + s
+                if s < 256:
+                    min_row(j)
+                if s > 0:
+                    sum_min(j - 1, qbank, s - 1)
+                if h == 0 and s == 4:
+                    split_e()
+                if h == 0 and s == 16:
+                    row_constants()
+                if h == 0 and s == 32:
+                    positives_diff()
+                if h == 0 and s == 48:
+                    row_constants_sum()
+                    positives_sum()
+            nc.scalar.copy(out=qs[:, :, 256 * h : 256 * (h + 1)], in_=qbank[:])
 
         def finish_store(ic):
             rows = slice(ic * P, (ic + 1) * P)
-            bank = turn_into_bank([acc_s[:, 0, rows], acc_s[:, 1, rows], acc_s[:, 2, rows], sums[:, rows]])
+            bank = turn_into_bank([uj[:, jc, rows] for jc in range(4)])
             res = fin.tile([P, NNEG + 1], F32, name="res%d" % ic)
-            nc.scalar.activation(out=res[:, 0:1], in_=sums[:, B + ic : B + ic + 1], func=ACT.Sqrt)
-            nc.scalar.activation(out=res[:, 1 : NNEG + 1], in_=bank[:], func=ACT.Sqrt)
+            nc.scalar.activation(out=res[:, 0:1], in_=psum_sq[:, ic : ic + 1], func=ACT.Sqrt)
+            nc.vector.tensor_tensor(out=qs[:, ic, :], in0=bank[:], in1=qs[:, ic, :], op=ALU.subtract)
+            nc.vector.tensor_scalar(
+                out=qs[:, ic, :], in0=qs[:, ic, :], scalar1=ki[:, ic : ic + 1], scalar2=0.0, op0=ALU.add, op1=ALU.max
+            )
+            nc.scalar.activation(out=res[:, 1 : NNEG + 1], in_=qs[:, ic, :], func=ACT.Sqrt)
             nc.vector.tensor_scalar_mul(out=res[:], in0=res[:], scalar1=-1.0)
             nc.sync.dma_start(out=out[rows, :], in_=res[:])
 
-        for s in range(B + 2):
-            if s < B:
-                relu_diff(s)
-            if 0 <= s - 1 < B:
-                turn(s - 1)
-            if 0 <= s - 2 < B:
-                reduce_row(s - 2)
-            if s == 6:
-                positives_diff()
-            if s == 8:
-                positives_sum()
-            if s == 12:
-                sums_from_stats(B, B + 2)
-            if s == P + 6:
-                sums_from_stats(0, P)
-            if s == P + 8:
-                finish_store(0)
-            if s == B - LATE_ROWS + 4:
-                sums_from_stats(P, B - LATE_ROWS)
-        sums_from_stats(B - LATE_ROWS, B)
+        for g in range(4):
+            abank = banks.tile([P, 4, 64, 2], F32, name="abank", tag="abank")
+            for s in range(65):
+                i = 64 * g + s
+                if s < 64:
+                    max_row(i)
+                if s > 0:
+                    sum_max(i - 1, abank, s - 1)
+                if g == 2 and s == 8:
+                    finish_store(0)
+            cols = slice(64 * g, 64 * (g + 1))
+            nc.vector.tensor_reduce(out=tj[:, :, cols], in_=abank[:], axis=mybir.AxisListType.X, op=ALU.add)
+            for jc in range(4):
+                nc.scalar.activation(
+                    out=uj[:, jc, cols], in_=tj[:, jc, cols], func=ACT.Identity, bias=nn[:, jc : jc + 1], scale=-1.0
+                )
         finish_store(1)

@@ -280,6 +280,13 @@ def tile_hypernymvisual_acc_kernel(tc, vfs, p_lfs, n_lfs, W_hidden, b_hidden, W_
                 nc.tensor.transpose(out=bank[:, c * P : (c + 1) * P], in_=pieces[c], identity=ident_f[:])
             return bank
 
+        wpool = ctx.enter_context(tc.psum_pool(name="wpool", bufs=1))
+        wbank = wpool.tile([P, 4, P], BF16)
+
+        def keep_warm(count):
+            for w in range(count):
+                nc.tensor.transpose(out=wbank[:, w % 4, :], in_=ident_b[:], identity=ident_b[:])
+
         q_tiles = {}
 
         def min_row(j):
@@ -358,6 +365,7 @@ def tile_hypernymvisual_acc_kernel(tc, vfs, p_lfs, n_lfs, W_hidden, b_hidden, W_
                     min_row(j)
                 if s > 0:
                     sum_min(j - 1, qbank, s - 1)
+                    keep_warm(2)
                 if h == 0 and s == 4:
                     split_e()
                 if h == 0 and s == 16:
@@ -390,6 +398,7 @@ def tile_hypernymvisual_acc_kernel(tc, vfs, p_lfs, n_lfs, W_hidden, b_hidden, W_
                     max_row(i)
                 if s > 0:
                     sum_max(i - 1, abank, s - 1)
+                    keep_warm(4)
                 if g == 2 and s == 8:
                     finish_store(0)
             cols = slice(64 * g, 64 * (g + 1))

@@ -17,6 +17,7 @@ FLOPS = 2 * B * VF * HID + 2 * B * HID * EMB + 4 * B * (NNEG + 1) * EMB
 
 W_BUFS = 6
 M_BUFS = 4
+NV = 384
 ROUND_ON_VECTOR = (3, 6, 7)
 
 
@@ -253,7 +254,9 @@ def tile_hypernymvisual_acc_kernel(tc, vfs, p_lfs, n_lfs, W_hidden, b_hidden, W_
 
         fin = ctx.enter_context(tc.tile_pool(name="fin", bufs=1))
         mpool = ctx.enter_context(tc.tile_pool(name="mpool", bufs=M_BUFS))
-        banks = ctx.enter_context(tc.psum_pool(name="banks", bufs=2))
+        banks = ctx.enter_context(tc.psum_pool(name="banks", bufs=4))
+        sbanks = ctx.enter_context(tc.psum_pool(name="sbanks", bufs=2))
+        wpool = ctx.enter_context(tc.psum_pool(name="wpool", bufs=1))
 
         ones = fin.tile([P, 2], F32)
         nc.vector.memset(ones[:], 1.0)
@@ -264,24 +267,24 @@ def tile_hypernymvisual_acc_kernel(tc, vfs, p_lfs, n_lfs, W_hidden, b_hidden, W_
         rp = fin.tile([P, 4, B], F32)
         nn = fin.tile([P, 4], F32)
         psum_sq = fin.tile([P, 2], F32)
-        qs = fin.tile([P, 2, NNEG], F32)
-        tj = fin.tile([P, 4, B], F32)
-        uj = fin.tile([P, 4, B], F32)
+        qs = fin.tile([P, 2, NV], F32)
+        tj = fin.tile([P, 3, B], F32)
+        uj = fin.tile([P, 3, B], F32)
+        accs = fin.tile([P, 2, NNEG - NV], F32)
+        wbank = wpool.tile([P, 4, P], BF16)
 
-        for jc in range(4):
-            junk = mpool.tile([P, EMB], F32, name="junk", tag="junk")
-            nc.scalar.activation(
-                out=junk[:], in_=nraw[:, jc * EMB : (jc + 1) * EMB], func=ACT.Square, accum_out=nn[:, jc : jc + 1]
-            )
+        def negative_norms():
+            for jc in range(3):
+                junk = mpool.tile([P, EMB], F32, name="junk", tag="junk")
+                nc.scalar.activation(
+                    out=junk[:], in_=nraw[:, jc * EMB : (jc + 1) * EMB], func=ACT.Square, accum_out=nn[:, jc : jc + 1]
+                )
 
         def turn_into_bank(pieces):
             bank = banks.tile([P, 4 * P], F32, name="bank", tag="bank")
-            for c in range(4):
+            for c in range(len(pieces)):
                 nc.tensor.transpose(out=bank[:, c * P : (c + 1) * P], in_=pieces[c], identity=ident_f[:])
             return bank
-
-        wpool = ctx.enter_context(tc.psum_pool(name="wpool", bufs=1))
-        wbank = wpool.tile([P, 4, P], BF16)
 
         def keep_warm(count):
             for w in range(count):
@@ -309,13 +312,13 @@ def tile_hypernymvisual_acc_kernel(tc, vfs, p_lfs, n_lfs, W_hidden, b_hidden, W_
         m_tiles = {}
 
         def max_row(i):
-            m = mpool.tile([P, 4, NNEG], BF16, name="m", tag="m")
+            m = mpool.tile([P, 4, NV], BF16, name="m", tag="m")
             for c in range(4):
-                nc.vector.tensor_scalar_max(out=m[:, c, :], in0=nT[:, c, :], scalar1=ehT[:, c, i : i + 1])
+                nc.vector.tensor_scalar_max(out=m[:, c, :], in0=nT[:, c, 0:NV], scalar1=ehT[:, c, i : i + 1])
             m_tiles[i] = m
 
         def sum_max(i, abank, col):
-            for jc in range(4):
+            for jc in range(3):
                 for c in range(4):
                     nc.tensor.matmul(
                         out=abank[:, jc, col, :],
@@ -324,6 +327,34 @@ def tile_hypernymvisual_acc_kernel(tc, vfs, p_lfs, n_lfs, W_hidden, b_hidden, W_
                         start=(c == 0),
                         stop=(c == 3),
                     )
+
+        r_tiles = {}
+        r_banks = {}
+
+        def scalar_relu(k):
+            r = mpool.tile([P, 4, B], F32, name="r", tag="r")
+            for c in range(4):
+                nc.scalar.activation(
+                    out=r[:, c, :], in_=eT[:, c, :], func=ACT.Relu, bias=nT[:, c, NV + k : NV + k + 1], scale=-1.0
+                )
+            r_tiles[k] = r
+
+        def scalar_turn(k):
+            r_banks[k] = [turn_into_bank([r_tiles[k][:, c, ic * P : (ic + 1) * P] for c in range(4)]) for ic in range(2)]
+
+        def scalar_square(k):
+            for ic in range(2):
+                junk = mpool.tile([P, EMB], F32, name="junk", tag="junk")
+                nc.scalar.activation(
+                    out=junk[:], in_=r_banks[k][ic][:], func=ACT.Square, accum_out=accs[:, ic, k : k + 1]
+                )
+
+        def scalar_step(k):
+            if k < NNEG - NV:
+                scalar_relu(k)
+            if 0 <= k - 1 < NNEG - NV:
+                scalar_turn(k - 1)
+                scalar_square(k - 1)
 
         def split_e():
             nc.vector.tensor_tensor(out=el[:], in0=eT[:], in1=ehT[:], op=ALU.subtract)
@@ -357,54 +388,68 @@ def tile_hypernymvisual_acc_kernel(tc, vfs, p_lfs, n_lfs, W_hidden, b_hidden, W_
                 junk = mpool.tile([P, EMB], F32, name="junk", tag="junk")
                 nc.scalar.activation(out=junk[:], in_=bank[:], func=ACT.Square, accum_out=psum_sq[:, ic : ic + 1])
 
-        for h in range(2):
-            qbank = banks.tile([P, 2, 256], F32, name="qbank", tag="qbank")
-            for s in range(257):
-                j = 256 * h + s
-                if s < 256:
-                    min_row(j)
-                if s > 0:
-                    sum_min(j - 1, qbank, s - 1)
-                    keep_warm(2)
-                if h == 0 and s == 4:
-                    split_e()
-                if h == 0 and s == 16:
-                    row_constants()
-                if h == 0 and s == 32:
-                    positives_diff()
-                if h == 0 and s == 48:
-                    row_constants_sum()
-                    positives_sum()
-            nc.scalar.copy(out=qs[:, :, 256 * h : 256 * (h + 1)], in_=qbank[:])
-
         def finish_store(ic):
             rows = slice(ic * P, (ic + 1) * P)
-            bank = turn_into_bank([uj[:, jc, rows] for jc in range(4)])
+            bank = turn_into_bank([uj[:, jc, rows] for jc in range(3)])
             res = fin.tile([P, NNEG + 1], F32, name="res%d" % ic)
             nc.scalar.activation(out=res[:, 0:1], in_=psum_sq[:, ic : ic + 1], func=ACT.Sqrt)
-            nc.vector.tensor_tensor(out=qs[:, ic, :], in0=bank[:], in1=qs[:, ic, :], op=ALU.subtract)
+            nc.scalar.activation(out=res[:, NV + 1 : NNEG + 1], in_=accs[:, ic, :], func=ACT.Sqrt)
+            nc.vector.tensor_tensor(out=qs[:, ic, :], in0=bank[:, 0:NV], in1=qs[:, ic, :], op=ALU.subtract)
             nc.vector.tensor_scalar(
                 out=qs[:, ic, :], in0=qs[:, ic, :], scalar1=ki[:, ic : ic + 1], scalar2=0.0, op0=ALU.add, op1=ALU.max
             )
-            nc.scalar.activation(out=res[:, 1 : NNEG + 1], in_=qs[:, ic, :], func=ACT.Sqrt)
+            nc.scalar.activation(out=res[:, 1 : NV + 1], in_=qs[:, ic, :], func=ACT.Sqrt)
             nc.vector.tensor_scalar_mul(out=res[:], in0=res[:], scalar1=-1.0)
             nc.sync.dma_start(out=out[rows, :], in_=res[:])
 
+        steps = 0
+        scalar_steps = 0
+        for h in range(2):
+            qbank = sbanks.tile([P, 2, NV // 2], F32, name="qbank", tag="sbank")
+            for s in range(NV // 2 + 1):
+                j = (NV // 2) * h + s
+                if s < NV // 2:
+                    min_row(j)
+                if s > 0:
+                    sum_min(j - 1, qbank, s - 1)
+                    keep_warm(1)
+                if steps % 5 == 0:
+                    scalar_step(scalar_steps)
+                    scalar_steps += 1
+                if steps == 4:
+                    split_e()
+                if steps == 16:
+                    row_constants()
+                if steps == 32:
+                    positives_diff()
+                if steps == 48:
+                    row_constants_sum()
+                    positives_sum()
+                if steps == 64:
+                    negative_norms()
+                steps += 1
+            nc.scalar.copy(out=qs[:, :, (NV // 2) * h : (NV // 2) * (h + 1)], in_=qbank[:])
         for g in range(4):
-            abank = banks.tile([P, 4, 64, 2], F32, name="abank", tag="abank")
+            abank = sbanks.tile([P, 3, 64, 2], F32, name="abank", tag="sbank")
             for s in range(65):
                 i = 64 * g + s
                 if s < 64:
                     max_row(i)
                 if s > 0:
                     sum_max(i - 1, abank, s - 1)
-                    keep_warm(4)
-                if g == 2 and s == 8:
-                    finish_store(0)
+                    keep_warm(1)
+                if steps % 5 == 0:
+                    scalar_step(scalar_steps)
+                    scalar_steps += 1
+                steps += 1
             cols = slice(64 * g, 64 * (g + 1))
             nc.vector.tensor_reduce(out=tj[:, :, cols], in_=abank[:], axis=mybir.AxisListType.X, op=ALU.add)
-            for jc in range(4):
+            for jc in range(3):
                 nc.scalar.activation(
                     out=uj[:, jc, cols], in_=tj[:, jc, cols], func=ACT.Identity, bias=nn[:, jc : jc + 1], scale=-1.0
                 )
+        while scalar_steps <= NNEG - NV:
+            scalar_step(scalar_steps)
+            scalar_steps += 1
+        finish_store(0)
         finish_store(1)

@@ -16,8 +16,9 @@ B, NNEG, VF, HID, EMB = 256, 512, 4096, 2048, 512
 FLOPS = 2 * B * VF * HID + 2 * B * HID * EMB + 4 * B * (NNEG + 1) * EMB
 
 W_BUFS = 6
-M_BUFS = 4
+M_BUFS = 6
 NV = 384
+ROWS_LATE = 3
 ROUND_ON_VECTOR = (3, 6, 7)
 
 
@@ -256,7 +257,6 @@ def tile_hypernymvisual_acc_kernel(tc, vfs, p_lfs, n_lfs, W_hidden, b_hidden, W_
         mpool = ctx.enter_context(tc.tile_pool(name="mpool", bufs=M_BUFS))
         banks = ctx.enter_context(tc.psum_pool(name="banks", bufs=4))
         sbanks = ctx.enter_context(tc.psum_pool(name="sbanks", bufs=2))
-        wpool = ctx.enter_context(tc.psum_pool(name="wpool", bufs=1))
 
         ones = fin.tile([P, 2], F32)
         nc.vector.memset(ones[:], 1.0)
@@ -271,11 +271,10 @@ def tile_hypernymvisual_acc_kernel(tc, vfs, p_lfs, n_lfs, W_hidden, b_hidden, W_
         tj = fin.tile([P, 3, B], F32)
         uj = fin.tile([P, 3, B], F32)
         accs = fin.tile([P, 2, NNEG - NV], F32)
-        wbank = wpool.tile([P, 4, P], BF16)
 
         def negative_norms():
             for jc in range(3):
-                junk = mpool.tile([P, EMB], F32, name="junk", tag="junk")
+                junk = mpool.tile([P, EMB], F32, name="junk", tag="junk", bufs=3)
                 nc.scalar.activation(
                     out=junk[:], in_=nraw[:, jc * EMB : (jc + 1) * EMB], func=ACT.Square, accum_out=nn[:, jc : jc + 1]
                 )
@@ -285,10 +284,6 @@ def tile_hypernymvisual_acc_kernel(tc, vfs, p_lfs, n_lfs, W_hidden, b_hidden, W_
             for c in range(len(pieces)):
                 nc.tensor.transpose(out=bank[:, c * P : (c + 1) * P], in_=pieces[c], identity=ident_f[:])
             return bank
-
-        def keep_warm(count):
-            for w in range(count):
-                nc.tensor.transpose(out=wbank[:, w % 4, :], in_=ident_b[:], identity=ident_b[:])
 
         q_tiles = {}
 
@@ -332,7 +327,7 @@ def tile_hypernymvisual_acc_kernel(tc, vfs, p_lfs, n_lfs, W_hidden, b_hidden, W_
         r_banks = {}
 
         def scalar_relu(k):
-            r = mpool.tile([P, 4, B], F32, name="r", tag="r")
+            r = mpool.tile([P, 4, B], F32, name="r", tag="r", bufs=3)
             for c in range(4):
                 nc.scalar.activation(
                     out=r[:, c, :], in_=eT[:, c, :], func=ACT.Relu, bias=nT[:, c, NV + k : NV + k + 1], scale=-1.0
@@ -344,7 +339,7 @@ def tile_hypernymvisual_acc_kernel(tc, vfs, p_lfs, n_lfs, W_hidden, b_hidden, W_
 
         def scalar_square(k):
             for ic in range(2):
-                junk = mpool.tile([P, EMB], F32, name="junk", tag="junk")
+                junk = mpool.tile([P, EMB], F32, name="junk", tag="junk", bufs=3)
                 nc.scalar.activation(
                     out=junk[:], in_=r_banks[k][ic][:], func=ACT.Square, accum_out=accs[:, ic, k : k + 1]
                 )
@@ -385,7 +380,7 @@ def tile_hypernymvisual_acc_kernel(tc, vfs, p_lfs, n_lfs, W_hidden, b_hidden, W_
         def positives_sum():
             for ic in range(2):
                 bank = turn_into_bank([rp[:, c, ic * P : (ic + 1) * P] for c in range(4)])
-                junk = mpool.tile([P, EMB], F32, name="junk", tag="junk")
+                junk = mpool.tile([P, EMB], F32, name="junk", tag="junk", bufs=3)
                 nc.scalar.activation(out=junk[:], in_=bank[:], func=ACT.Square, accum_out=psum_sq[:, ic : ic + 1])
 
         def finish_store(ic):
@@ -402,54 +397,62 @@ def tile_hypernymvisual_acc_kernel(tc, vfs, p_lfs, n_lfs, W_hidden, b_hidden, W_
             nc.vector.tensor_scalar_mul(out=res[:], in0=res[:], scalar1=-1.0)
             nc.sync.dma_start(out=out[rows, :], in_=res[:])
 
-        steps = 0
-        scalar_steps = 0
-        for h in range(2):
-            qbank = sbanks.tile([P, 2, NV // 2], F32, name="qbank", tag="sbank")
-            for s in range(NV // 2 + 1):
-                j = (NV // 2) * h + s
-                if s < NV // 2:
-                    min_row(j)
-                if s > 0:
-                    sum_min(j - 1, qbank, s - 1)
-                    keep_warm(1)
-                if steps % 5 == 0:
-                    scalar_step(scalar_steps)
-                    scalar_steps += 1
-                if steps == 4:
-                    split_e()
-                if steps == 16:
-                    row_constants()
-                if steps == 32:
-                    positives_diff()
-                if steps == 48:
-                    row_constants_sum()
-                    positives_sum()
-                if steps == 64:
-                    negative_norms()
-                steps += 1
-            nc.scalar.copy(out=qs[:, :, (NV // 2) * h : (NV // 2) * (h + 1)], in_=qbank[:])
-        for g in range(4):
-            abank = sbanks.tile([P, 3, 64, 2], F32, name="abank", tag="sbank")
-            for s in range(65):
-                i = 64 * g + s
-                if s < 64:
-                    max_row(i)
-                if s > 0:
-                    sum_max(i - 1, abank, s - 1)
-                    keep_warm(1)
-                if steps % 5 == 0:
-                    scalar_step(scalar_steps)
-                    scalar_steps += 1
-                steps += 1
-            cols = slice(64 * g, 64 * (g + 1))
-            nc.vector.tensor_reduce(out=tj[:, :, cols], in_=abank[:], axis=mybir.AxisListType.X, op=ALU.add)
-            for jc in range(3):
-                nc.scalar.activation(
-                    out=uj[:, jc, cols], in_=tj[:, jc, cols], func=ACT.Identity, bias=nn[:, jc : jc + 1], scale=-1.0
-                )
-        while scalar_steps <= NNEG - NV:
-            scalar_step(scalar_steps)
-            scalar_steps += 1
+        q_state = {}
+        a_state = {}
+
+        def min_step(j):
+            h, col = divmod(j, NV // 2)
+            min_row(j)
+            if col == 0:
+                q_state[h] = sbanks.tile([P, 2, NV // 2], F32, name="qbank", tag="qbank")
+            return lambda: min_sums(j, h, col)
+
+        def min_sums(j, h, col):
+            sum_min(j, q_state[h], col)
+            if col == NV // 2 - 1:
+                nc.scalar.copy(out=qs[:, :, (NV // 2) * h : (NV // 2) * (h + 1)], in_=q_state[h][:])
+
+        def max_step(i):
+            g, col = divmod(i, 64)
+            max_row(i)
+            if col == 0:
+                a_state[g] = sbanks.tile([P, 3, 64, 2], F32, name="abank", tag="abank")
+            return lambda: max_sums(i, g, col)
+
+        def max_sums(i, g, col):
+            sum_max(i, a_state[g], col)
+            if col == 63:
+                cols = slice(64 * g, 64 * (g + 1))
+                nc.vector.tensor_reduce(out=tj[:, :, cols], in_=a_state[g][:], axis=mybir.AxisListType.X, op=ALU.add)
+                for jc in range(3):
+                    nc.scalar.activation(
+                        out=uj[:, jc, cols], in_=tj[:, jc, cols], func=ACT.Identity, bias=nn[:, jc : jc + 1], scale=-1.0
+                    )
+
+        last = None
+        for k in range(NNEG - NV + ROWS_LATE + 1):
+            scalar_step(k)
+            units = []
+            if k < NNEG - NV:
+                units += [(min_step, 3 * k + t) for t in range(3)]
+            if 0 <= k - ROWS_LATE < NNEG - NV:
+                units += [(max_step, 2 * (k - ROWS_LATE) + t) for t in range(2)]
+            for step, index in units:
+                sums = step(index)
+                if last is not None:
+                    last()
+                last = sums
+            if k == 0:
+                split_e()
+            if k == 6:
+                row_constants()
+            if k == 10:
+                positives_diff()
+            if k == 14:
+                row_constants_sum()
+                positives_sum()
+            if k == 18:
+                negative_norms()
+        last()
         finish_store(0)
         finish_store(1)

@@ -15,7 +15,7 @@ P = 128
 B, NNEG, VF, HID, EMB = 256, 512, 4096, 2048, 512
 FLOPS = 2 * B * VF * HID + 2 * B * HID * EMB + 4 * B * (NNEG + 1) * EMB
 
-W_BUFS = 6
+W_BUFS = 8
 M_BUFS = 6
 NV = 384
 ROWS_LATE = 3
@@ -36,10 +36,12 @@ def tile_hypernymvisual_acc_kernel(tc, vfs, p_lfs, n_lfs, W_hidden, b_hidden, W_
         eT = keep.tile([P, 4, B], F32)
         ehT = keep.tile([P, 4, B], BF16)
         nraw = keep.tile([P, 4 * EMB], BF16)
-        bias = keep.tile([P, 32], F32)
+        bias = keep.tile([P, 3, 8], F32)
         one = keep.tile([P, 1], F32)
         nc.vector.memset(one[:], 1.0)
         warm = keep.tile([P, 1], F32)
+
+        praw = keep.tile([P, 2 * EMB], BF16)
 
         with ExitStack() as mx:
             fix = mx.enter_context(tc.tile_pool(name="fix", bufs=1))
@@ -54,41 +56,43 @@ def tile_hypernymvisual_acc_kernel(tc, vfs, p_lfs, n_lfs, W_hidden, b_hidden, W_
                 else:
                     nc.scalar.copy(out=dst, in_=src)
 
-            brow = fix.tile([P, P], BF16)
+            brow = fix.tile([P, 3 * P], BF16)
             nc.vector.memset(brow[:], 0.0)
-            nc.scalar.dma_start(out=brow[0:16, :], in_=b_hidden.rearrange("(r c) -> r c", c=P))
-            nc.scalar.dma_start(out=brow[16:20, :], in_=b_embed.rearrange("(r c) -> r c", c=P))
+            nc.scalar.dma_start(out=brow[0:8, 0 : 2 * P], in_=b_hidden.rearrange("(r c) -> r c", c=2 * P))
+            nc.scalar.dma_start(out=brow[0:4, 2 * P : 3 * P], in_=b_embed.rearrange("(r c) -> r c", c=P))
             nc.scalar.activation(out=warm[:], in_=one[:], func=ACT.Sqrt)
             vraw = []
             for bc in range(2):
                 t = fix.tile([P, VF], BF16, name="vraw%d" % bc)
-                nc.sync.dma_start(out=t[:], in_=vfs[bc * P : (bc + 1) * P, :])
+                for half in range(2):
+                    cols = slice(half * VF // 2, (half + 1) * VF // 2)
+                    nc.sync.dma_start(out=t[:, cols], in_=vfs[bc * P : (bc + 1) * P, cols])
                 vraw.append(t)
             weraw = fix.tile([P, 4 * HID], BF16)
-            praw = fix.tile([P, 2 * EMB], BF16)
             wraws = []
+            w_rows = W_hidden.rearrange("(g u m e) k -> g u e m k", g=4, u=2, m=P, e=2)
 
             def load_w(hc):
                 t = raws.tile([P, VF], BF16, name="wraw", tag="wraw")
-                nc.sync.dma_start(out=t[:], in_=W_hidden[hc * P : (hc + 1) * P, :])
+                nc.sync.dma_start(out=t[:], in_=w_rows[hc // 4, (hc // 2) % 2, hc % 2])
                 wraws.append(t)
 
-            for hc in range(4):
-                load_w(hc)
-            nc.sync.dma_start(
-                out=weraw[:].rearrange("p (c k) -> p c k", c=4), in_=W_embed.rearrange("(c p) k -> p c k", p=P)
-            )
-            nc.sync.dma_start(
-                out=nraw[:].rearrange("p (c k) -> p c k", c=4), in_=n_lfs.rearrange("(c p) k -> p c k", p=P)
-            )
-            nc.sync.dma_start(
-                out=praw[:].rearrange("p (c k) -> p c k", c=2), in_=p_lfs.rearrange("(c p) k -> p c k", p=P)
-            )
-            for hc in range(4, W_BUFS):
+            for hc in range(W_BUFS):
                 load_w(hc)
 
-            def turn_words(words, dst_of_q, vector_banks, first_bank):
-                for q in range(4):
+            def load_side():
+                nc.sync.dma_start(
+                    out=weraw[:].rearrange("p (c k) -> p c k", c=4), in_=W_embed.rearrange("(c p) k -> p c k", p=P)
+                )
+                nc.sync.dma_start(
+                    out=nraw[:].rearrange("p (c k) -> p c k", c=4), in_=n_lfs.rearrange("(c p) k -> p c k", p=P)
+                )
+                nc.sync.dma_start(
+                    out=praw[:].rearrange("p (c k) -> p c k", c=2), in_=p_lfs.rearrange("(c p) k -> p c k", p=P)
+                )
+
+            def turn_words(words, banks_of, dst_of_q, vector_banks, first_bank):
+                for q in banks_of:
                     xt = ps_t.tile([P, 2, 2, P], F32, name="xt", tag="xt")
                     for gg in range(2):
                         for u in range(2):
@@ -103,14 +107,13 @@ def tile_hypernymvisual_acc_kernel(tc, vfs, p_lfs, n_lfs, W_hidden, b_hidden, W_
             for bc in range(2):
                 turn_words(
                     vraw[bc][:].bitcast(F32),
+                    range(4),
                     lambda q: vgrp_w[:, 2 * q : 2 * q + 2, bc * P : (bc + 1) * P, :],
                     (0, 2, 4, 6),
                     4 * bc,
                 )
-            bt = ps_t.tile([P, P], BF16, name="bt", tag="xt")
-            nc.tensor.transpose(out=bt[:], in_=brow[:], identity=ident_b[:])
-            nc.vector.tensor_copy(out=bias[:], in_=bt[:, 0:32])
-            for h in range(2):
+
+            def quantise_v(h):
                 nc.vector.quantize_mx(
                     out=vcodes[:, 1024 * h : 1024 * (h + 1)].bitcast(FP8X4),
                     scales=vscales[:, 1024 * h : 1024 * (h + 1)],
@@ -122,23 +125,27 @@ def tile_hypernymvisual_acc_kernel(tc, vfs, p_lfs, n_lfs, W_hidden, b_hidden, W_
             hcodes = fix.tile([P, 4 * B], U32, align_bytes=64)
             hscales = fix.tile([P, 4 * B], U8, align_bytes=64)
             egrp = fix.tile([P, 4 * EMB * 4], BF16, align_bytes=64)
-            egrp_v = egrp[:].rearrange("p (g d t) -> p g d t", g=4, d=EMB, t=4)
+            egrp_w = egrp[:].bitcast(F32).rearrange("p (g d u) -> p g d u", g=4, d=EMB, u=2)
             ecodes = fix.tile([P, 4 * EMB], U32, align_bytes=64)
             escales = fix.tile([P, 4 * EMB], U8, align_bytes=64)
 
-            def side_turns():
-                for dc in range(4):
-                    for gh in range(2):
-                        xb = ps_t.tile([P, 2, 4, P], BF16, name="xb", tag="xt")
-                        for gg in range(2):
-                            for t in range(4):
-                                lo = dc * HID + 512 * (2 * gh + gg) + P * t
-                                nc.tensor.transpose(out=xb[:, gg, t, :], in_=weraw[:, lo : lo + P], identity=ident_b[:])
-                        copy_out(
-                            gh == 1,
-                            egrp_v[:, 2 * gh : 2 * gh + 2, dc * P : (dc + 1) * P, :],
-                            xb[:].rearrange("p g t r -> p g r t"),
-                        )
+            def turn_bias():
+                bt = ps_t.tile([P, 3, P], BF16, name="bt", tag="xt")
+                for e in range(2):
+                    nc.tensor.transpose(out=bt[:, e, :], in_=brow[:, e : 2 * P : 2], identity=ident_b[:])
+                nc.tensor.transpose(out=bt[:, 2, :], in_=brow[:, 2 * P : 3 * P], identity=ident_b[:])
+                nc.vector.tensor_copy(out=bias[:], in_=bt[:, :, 0:8])
+
+            def turn_embed(dc):
+                turn_words(
+                    weraw[:, dc * HID : (dc + 1) * HID].bitcast(F32),
+                    range(2),
+                    lambda q: egrp_w[:, 2 * q : 2 * q + 2, dc * P : (dc + 1) * P, :],
+                    (1, 3),
+                    0,
+                )
+
+            def turn_negatives():
                 for ch in range(2):
                     nb = ps_t.tile([P, 2, NNEG], BF16, name="nb", tag="xt")
                     for cc in range(2):
@@ -147,23 +154,14 @@ def tile_hypernymvisual_acc_kernel(tc, vfs, p_lfs, n_lfs, W_hidden, b_hidden, W_
                             nc.tensor.transpose(
                                 out=nb[:, cc, jc * P : (jc + 1) * P], in_=nraw[:, lo : lo + P], identity=ident_b[:]
                             )
-                    copy_out(ch == 1, nT[:, 2 * ch : 2 * ch + 2, :], nb[:])
-                pb = ps_t.tile([P, 4, B], BF16, name="pb", tag="xt")
-                for c in range(4):
-                    for ic in range(2):
-                        lo = ic * EMB + c * P
-                        nc.tensor.transpose(
-                            out=pb[:, c, ic * P : (ic + 1) * P], in_=praw[:, lo : lo + P], identity=ident_b[:]
-                        )
-                copy_out(False, pT[:], pb[:])
+                    copy_out(False, nT[:, 2 * ch : 2 * ch + 2, :], nb[:])
 
-            def side_quantise():
-                for h in range(2):
-                    nc.vector.quantize_mx(
-                        out=ecodes[:, 1024 * h : 1024 * (h + 1)].bitcast(FP8X4),
-                        scales=escales[:, 1024 * h : 1024 * (h + 1)],
-                        in_=egrp[:, 4096 * h : 4096 * (h + 1)],
-                    )
+            def quantise_embed(h):
+                nc.vector.quantize_mx(
+                    out=ecodes[:, 1024 * h : 1024 * (h + 1)].bitcast(FP8X4),
+                    scales=escales[:, 1024 * h : 1024 * (h + 1)],
+                    in_=egrp[:, 4096 * h : 4096 * (h + 1)],
+                )
 
             wgrps = {}
             wq = {}
@@ -173,6 +171,7 @@ def tile_hypernymvisual_acc_kernel(tc, vfs, p_lfs, n_lfs, W_hidden, b_hidden, W_
                 wgrp_w = wgrp[:].bitcast(F32).rearrange("p (g r u) -> p g r u", g=8, r=P, u=2)
                 turn_words(
                     wraws[hc][:].bitcast(F32),
+                    range(4),
                     lambda q: wgrp_w[:, 2 * q : 2 * q + 2, :, :],
                     ROUND_ON_VECTOR,
                     4 * (hc % 2),
@@ -180,6 +179,8 @@ def tile_hypernymvisual_acc_kernel(tc, vfs, p_lfs, n_lfs, W_hidden, b_hidden, W_
                 wgrps[hc] = wgrp
                 if hc + W_BUFS < 16:
                     load_w(hc + W_BUFS)
+                    if hc + W_BUFS == 15:
+                        load_side()
 
             def quantise_w(hc):
                 wcodes = work.tile([P, 1024], U32, name="wcodes", tag="wcodes", align_bytes=64)
@@ -201,7 +202,11 @@ def tile_hypernymvisual_acc_kernel(tc, vfs, p_lfs, n_lfs, W_hidden, b_hidden, W_
                         stop=(g == 7),
                     )
                 nc.scalar.activation(
-                    out=hgrp_v[:, hc // 4, :, hc % 4], in_=acc[:], func=ACT.Identity, bias=bias[:, hc : hc + 1], scale=1.0
+                    out=hgrp_v[:, hc // 4, :, hc % 4],
+                    in_=acc[:],
+                    func=ACT.Identity,
+                    bias=bias[:, hc % 2, hc // 2 : hc // 2 + 1],
+                    scale=1.0,
                 )
 
             def quantise_h(g2):
@@ -211,36 +216,47 @@ def tile_hypernymvisual_acc_kernel(tc, vfs, p_lfs, n_lfs, W_hidden, b_hidden, W_
                     in_=hgrp[:, 4 * B * g2 : 4 * B * (g2 + 1)],
                 )
 
+            quantise_v(0)
             turn_w(0)
+            quantise_v(1)
             quantise_w(0)
+            turn_bias()
             for hc in range(1, 4):
                 turn_w(hc)
                 layer1(hc - 1)
                 quantise_w(hc)
-            side_turns()
-            layer1(3)
-            side_quantise()
-            quantise_h(0)
             for rnd in range(2, 8):
+                if rnd == 7:
+                    for dc in range(4):
+                        turn_embed(dc)
                 turn_w(2 * rnd)
                 turn_w(2 * rnd + 1)
-                if rnd > 2:
+                if rnd == 2:
+                    layer1(3)
+                else:
                     layer1(2 * rnd - 2)
                     layer1(2 * rnd - 1)
                 quantise_w(2 * rnd)
                 quantise_w(2 * rnd + 1)
-                if rnd > 2 and rnd % 2 == 0:
-                    quantise_h(rnd // 2 - 1)
+                if rnd == 3:
+                    quantise_h(0)
+                if rnd == 5:
+                    quantise_h(1)
+                if rnd == 7:
+                    quantise_embed(0)
+                    quantise_embed(1)
+                    quantise_h(2)
+            turn_negatives()
             layer1(14)
             layer1(15)
             quantise_h(3)
 
-            for dc in range(4):
-                acc = ps_a.tile([P, B], F32, name="acc", tag="acc")
-                for g2 in range(4):
+            accs2 = [ps_t.tile([P, B], F32, name="acc2", tag="xt") for dc in range(4)]
+            for g2 in range(4):
+                for dc in range(4):
                     lo = EMB * g2 + P * dc
                     nc.tensor.matmul_mx(
-                        out=acc[:],
+                        out=accs2[dc][:],
                         lhsT=ecodes[:, lo : lo + P].bitcast(FP8X4),
                         lhsT_scale=escales[:, lo : lo + P],
                         rhs=hcodes[:, B * g2 : B * (g2 + 1)].bitcast(FP8X4),
@@ -248,10 +264,11 @@ def tile_hypernymvisual_acc_kernel(tc, vfs, p_lfs, n_lfs, W_hidden, b_hidden, W_
                         start=(g2 == 0),
                         stop=(g2 == 3),
                     )
+            for dc in range(4):
+                nc.vector.tensor_scalar_add(out=ehT[:, dc, :], in0=accs2[dc][:], scalar1=bias[:, 2, dc : dc + 1])
                 nc.scalar.activation(
-                    out=eT[:, dc, :], in_=acc[:], func=ACT.Identity, bias=bias[:, 16 + dc : 17 + dc], scale=1.0
+                    out=eT[:, dc, :], in_=accs2[dc][:], func=ACT.Identity, bias=bias[:, 2, dc : dc + 1], scale=1.0
                 )
-                nc.vector.tensor_copy(out=ehT[:, dc, :], in_=eT[:, dc, :])
 
         fin = ctx.enter_context(tc.tile_pool(name="fin", bufs=1))
         mpool = ctx.enter_context(tc.tile_pool(name="mpool", bufs=M_BUFS))
@@ -324,7 +341,6 @@ def tile_hypernymvisual_acc_kernel(tc, vfs, p_lfs, n_lfs, W_hidden, b_hidden, W_
                     )
 
         r_tiles = {}
-        r_banks = {}
 
         def scalar_relu(k):
             r = mpool.tile([P, 4, B], F32, name="r", tag="r", bufs=3)
@@ -334,22 +350,10 @@ def tile_hypernymvisual_acc_kernel(tc, vfs, p_lfs, n_lfs, W_hidden, b_hidden, W_
                 )
             r_tiles[k] = r
 
-        def scalar_turn(k):
-            r_banks[k] = [turn_into_bank([r_tiles[k][:, c, ic * P : (ic + 1) * P] for c in range(4)]) for ic in range(2)]
-
-        def scalar_square(k):
-            for ic in range(2):
-                junk = mpool.tile([P, EMB], F32, name="junk", tag="junk", bufs=3)
-                nc.scalar.activation(
-                    out=junk[:], in_=r_banks[k][ic][:], func=ACT.Square, accum_out=accs[:, ic, k : k + 1]
-                )
-
-        def scalar_step(k):
-            if k < NNEG - NV:
-                scalar_relu(k)
-            if 0 <= k - 1 < NNEG - NV:
-                scalar_turn(k - 1)
-                scalar_square(k - 1)
+        def scalar_square(k, ic):
+            bank = turn_into_bank([r_tiles[k][:, c, ic * P : (ic + 1) * P] for c in range(4)])
+            junk = mpool.tile([P, EMB], F32, name="junk", tag="junk", bufs=3)
+            nc.scalar.activation(out=junk[:], in_=bank[:], func=ACT.Square, accum_out=accs[:, ic, k : k + 1])
 
         def split_e():
             nc.vector.tensor_tensor(out=el[:], in0=eT[:], in1=ehT[:], op=ALU.subtract)
@@ -372,6 +376,16 @@ def tile_hypernymvisual_acc_kernel(tc, vfs, p_lfs, n_lfs, W_hidden, b_hidden, W_
                         stop=(c == 3),
                     )
             nc.vector.tensor_copy(out=ki[:], in_=kbank[:, :, 0])
+
+        def turn_positives():
+            pb = banks.tile([P, 4, B], BF16, name="pb", tag="bank")
+            for c in range(4):
+                for ic in range(2):
+                    lo = ic * EMB + c * P
+                    nc.tensor.transpose(
+                        out=pb[:, c, ic * P : (ic + 1) * P], in_=praw[:, lo : lo + P], identity=ident_b[:]
+                    )
+            nc.scalar.copy(out=pT[:], in_=pb[:])
 
         def positives_diff():
             nc.vector.tensor_tensor(out=rp[:], in0=pT[:], in1=eT[:], op=ALU.subtract)
@@ -399,6 +413,7 @@ def tile_hypernymvisual_acc_kernel(tc, vfs, p_lfs, n_lfs, W_hidden, b_hidden, W_
 
         q_state = {}
         a_state = {}
+        spare = []
 
         def min_step(j):
             h, col = divmod(j, NV // 2)
@@ -415,37 +430,53 @@ def tile_hypernymvisual_acc_kernel(tc, vfs, p_lfs, n_lfs, W_hidden, b_hidden, W_
         def max_step(i):
             g, col = divmod(i, 64)
             max_row(i)
-            if col == 0:
-                a_state[g] = sbanks.tile([P, 3, 64, 2], F32, name="abank", tag="abank")
             return lambda: max_sums(i, g, col)
+
+        def open_abank(g):
+            abank = sbanks.tile([P, 512], F32, name="abank", tag="abank")
+            a_state[g] = abank[:, 0:NV].rearrange("p (j i t) -> p j i t", j=3, i=64, t=2)
+            spare.append(abank[:, 448:512].bitcast(BF16))
+
+        def keep_warm(count):
+            for w in range(count):
+                nc.tensor.transpose(out=spare[-1], in_=ident_b[:], identity=ident_b[:])
 
         def max_sums(i, g, col):
             sum_max(i, a_state[g], col)
             if col == 63:
+                if g < 3:
+                    open_abank(g + 1)
                 cols = slice(64 * g, 64 * (g + 1))
-                nc.vector.tensor_reduce(out=tj[:, :, cols], in_=a_state[g][:], axis=mybir.AxisListType.X, op=ALU.add)
+                nc.vector.tensor_reduce(out=tj[:, :, cols], in_=a_state[g], axis=mybir.AxisListType.X, op=ALU.add)
                 for jc in range(3):
                     nc.scalar.activation(
                         out=uj[:, jc, cols], in_=tj[:, jc, cols], func=ACT.Identity, bias=nn[:, jc : jc + 1], scale=-1.0
                     )
 
+        open_abank(0)
         last = None
         for k in range(NNEG - NV + ROWS_LATE + 1):
-            scalar_step(k)
+            if k < NNEG - NV:
+                scalar_relu(k)
             units = []
             if k < NNEG - NV:
                 units += [(min_step, 3 * k + t) for t in range(3)]
             if 0 <= k - ROWS_LATE < NNEG - NV:
                 units += [(max_step, 2 * (k - ROWS_LATE) + t) for t in range(2)]
-            for step, index in units:
+            for turn, (step, index) in enumerate(units):
                 sums = step(index)
                 if last is not None:
                     last()
                 last = sums
+                if 0 <= k - 1 < NNEG - NV and turn < 2:
+                    scalar_square(k - 1, turn)
+                keep_warm(2 if turn in (2, 4) else 1)
             if k == 0:
                 split_e()
             if k == 6:
                 row_constants()
+            if k == 8:
+                turn_positives()
             if k == 10:
                 positives_diff()
             if k == 14:

@@ -16,9 +16,8 @@ B, NNEG, VF, HID, EMB = 256, 512, 4096, 2048, 512
 FLOPS = 2 * B * VF * HID + 2 * B * HID * EMB + 4 * B * (NNEG + 1) * EMB
 
 W_BUFS = 8
-M_BUFS = 6
-NV = 384
-ROWS_LATE = 3
+M_BUFS = 8
+OUT_LATE = 4
 ROUND_ON_VECTOR = (3, 6, 7)
 
 
@@ -32,9 +31,10 @@ def tile_hypernymvisual_acc_kernel(tc, vfs, p_lfs, n_lfs, W_hidden, b_hidden, W_
         ident_b = keep.tile([P, P], BF16)
         make_identity(nc, ident_b[:])
         nT = keep.tile([P, 4, NNEG], BF16)
-        pT = keep.tile([P, 4, B], F32)
-        eT = keep.tile([P, 4, B], F32)
-        ehT = keep.tile([P, 4, B], BF16)
+        e2T = keep.tile([P, 4, B], F32)
+        eh2 = keep.tile([P, 2, 4, B], BF16)
+        ehT = eh2[:, 0]
+        bias2 = keep.tile([P, 4], F32)
         nraw = keep.tile([P, 4 * EMB], BF16)
         bias = keep.tile([P, 3, 8], F32)
         one = keep.tile([P, 1], F32)
@@ -135,6 +135,7 @@ def tile_hypernymvisual_acc_kernel(tc, vfs, p_lfs, n_lfs, W_hidden, b_hidden, W_
                     nc.tensor.transpose(out=bt[:, e, :], in_=brow[:, e : 2 * P : 2], identity=ident_b[:])
                 nc.tensor.transpose(out=bt[:, 2, :], in_=brow[:, 2 * P : 3 * P], identity=ident_b[:])
                 nc.vector.tensor_copy(out=bias[:], in_=bt[:, :, 0:8])
+                nc.vector.tensor_scalar_mul(out=bias2[:], in0=bt[:, 2, 0:4], scalar1=2.0)
 
             def turn_embed(dc):
                 turn_words(
@@ -264,45 +265,52 @@ def tile_hypernymvisual_acc_kernel(tc, vfs, p_lfs, n_lfs, W_hidden, b_hidden, W_
                         start=(g2 == 0),
                         stop=(g2 == 3),
                     )
+            first_warm = ps_a.tile([P, P], BF16, name="first_warm", tag="acc")
+            for w in range(20):
+                nc.tensor.transpose(out=first_warm[:], in_=ident_b[:], identity=ident_b[:])
             for dc in range(4):
                 nc.vector.tensor_scalar_add(out=ehT[:, dc, :], in0=accs2[dc][:], scalar1=bias[:, 2, dc : dc + 1])
                 nc.scalar.activation(
-                    out=eT[:, dc, :], in_=accs2[dc][:], func=ACT.Identity, bias=bias[:, 2, dc : dc + 1], scale=1.0
+                    out=e2T[:, dc, :], in_=accs2[dc][:], func=ACT.Identity, bias=bias2[:, dc : dc + 1], scale=2.0
                 )
 
         fin = ctx.enter_context(tc.tile_pool(name="fin", bufs=1))
         mpool = ctx.enter_context(tc.tile_pool(name="mpool", bufs=M_BUFS))
         banks = ctx.enter_context(tc.psum_pool(name="banks", bufs=4))
         sbanks = ctx.enter_context(tc.psum_pool(name="sbanks", bufs=2))
+        wpool = ctx.enter_context(tc.psum_pool(name="wpool", bufs=1))
 
-        ones = fin.tile([P, 2], F32)
-        nc.vector.memset(ones[:], 1.0)
-        el = fin.tile([P, 4, B], F32)
-        w2 = fin.tile([P, 4, B, 2], BF16)
-        kk = fin.tile([P, 4, B], F32)
+        signs = fin.tile([P, 2], F32)
+        nc.vector.memset(signs[:, 0:1], 1.0)
+        nc.vector.memset(signs[:, 1:2], -1.0)
+        squares = fin.tile([P, 2, 4, B], F32)
         ki = fin.tile([P, 2], F32)
         rp = fin.tile([P, 4, B], F32)
         nn = fin.tile([P, 4], F32)
         psum_sq = fin.tile([P, 2], F32)
-        qs = fin.tile([P, 2, NV], F32)
-        tj = fin.tile([P, 3, B], F32)
-        uj = fin.tile([P, 3, B], F32)
-        accs = fin.tile([P, 2, NNEG - NV], F32)
+        qs = fin.tile([P, 2, NNEG], F32)
+        tj = fin.tile([P, 4, B], F32)
+        uj = fin.tile([P, 4, B], F32)
+        wbank = wpool.tile([P, 4, P], BF16)
 
-        def negative_norms():
-            for jc in range(3):
-                junk = mpool.tile([P, EMB], F32, name="junk", tag="junk", bufs=3)
-                nc.scalar.activation(
-                    out=junk[:], in_=nraw[:, jc * EMB : (jc + 1) * EMB], func=ACT.Square, accum_out=nn[:, jc : jc + 1]
-                )
+        def keep_warm(count):
+            for w in range(count):
+                nc.tensor.transpose(out=wbank[:, w % 4, :], in_=ident_b[:], identity=ident_b[:])
 
         def turn_into_bank(pieces):
             bank = banks.tile([P, 4 * P], F32, name="bank", tag="bank")
-            for c in range(len(pieces)):
+            for c in range(4):
                 nc.tensor.transpose(out=bank[:, c * P : (c + 1) * P], in_=pieces[c], identity=ident_f[:])
             return bank
 
+        def square_sum(src, dst):
+            junk = mpool.tile([P, EMB], F32, name="junk", tag="junk", bufs=2)
+            nc.scalar.activation(out=junk[:], in_=src, func=ACT.Square, accum_out=dst)
+
         q_tiles = {}
+        m_tiles = {}
+        q_banks = {}
+        a_banks = {}
 
         def min_row(j):
             q = mpool.tile([P, 4, B], BF16, name="q", tag="q")
@@ -310,180 +318,139 @@ def tile_hypernymvisual_acc_kernel(tc, vfs, p_lfs, n_lfs, W_hidden, b_hidden, W_
                 nc.vector.tensor_scalar_min(out=q[:, c, :], in0=ehT[:, c, :], scalar1=nT[:, c, j : j + 1])
             q_tiles[j] = q
 
-        def sum_min(j, qbank, col):
+        def min_sums(j):
+            h, col = divmod(j, NNEG // 2)
+            if col == 0:
+                q_banks[h] = sbanks.tile([P, 2, NNEG // 2], F32, name="qbank", tag="sbank")
             for ic in range(2):
                 for c in range(4):
                     nc.tensor.matmul(
-                        out=qbank[:, ic, col : col + 1],
+                        out=q_banks[h][:, ic, col : col + 1],
                         lhsT=q_tiles[j][:, c, ic * P : (ic + 1) * P],
                         rhs=nT[:, c, j : j + 1],
                         start=(c == 0),
                         stop=(c == 3),
                     )
+            keep_warm(1 + j % 2)
 
-        m_tiles = {}
+        def min_out(h):
+            nc.scalar.copy(out=qs[:, :, (NNEG // 2) * h : (NNEG // 2) * (h + 1)], in_=q_banks[h][:])
 
         def max_row(i):
-            m = mpool.tile([P, 4, NV], BF16, name="m", tag="m")
+            m = mpool.tile([P, 4, NNEG], BF16, name="m", tag="m")
             for c in range(4):
-                nc.vector.tensor_scalar_max(out=m[:, c, :], in0=nT[:, c, 0:NV], scalar1=ehT[:, c, i : i + 1])
+                nc.vector.tensor_scalar_max(out=m[:, c, :], in0=nT[:, c, :], scalar1=ehT[:, c, i : i + 1])
             m_tiles[i] = m
 
-        def sum_max(i, abank, col):
-            for jc in range(3):
+        def max_sums(i):
+            g, col = divmod(i, 64)
+            if col == 0:
+                a_banks[g] = sbanks.tile([P, 4, 64, 2], F32, name="abank", tag="sbank")
+            for jc in range(4):
                 for c in range(4):
                     nc.tensor.matmul(
-                        out=abank[:, jc, col, :],
+                        out=a_banks[g][:, jc, col, :],
                         lhsT=m_tiles[i][:, c, jc * P : (jc + 1) * P],
-                        rhs=w2[:, c, i, :],
+                        rhs=eh2[:, :, c, i],
                         start=(c == 0),
                         stop=(c == 3),
                     )
+            keep_warm(3)
 
-        r_tiles = {}
-
-        def scalar_relu(k):
-            r = mpool.tile([P, 4, B], F32, name="r", tag="r", bufs=3)
-            for c in range(4):
+        def max_out(g):
+            cols = slice(64 * g, 64 * (g + 1))
+            nc.vector.tensor_reduce(out=tj[:, :, cols], in_=a_banks[g][:], axis=mybir.AxisListType.X, op=ALU.add)
+            for jc in range(4):
                 nc.scalar.activation(
-                    out=r[:, c, :], in_=eT[:, c, :], func=ACT.Relu, bias=nT[:, c, NV + k : NV + k + 1], scale=-1.0
+                    out=uj[:, jc, cols], in_=tj[:, jc, cols], func=ACT.Identity, bias=nn[:, jc : jc + 1], scale=-1.0
                 )
-            r_tiles[k] = r
 
-        def scalar_square(k, ic):
-            bank = turn_into_bank([r_tiles[k][:, c, ic * P : (ic + 1) * P] for c in range(4)])
-            junk = mpool.tile([P, EMB], F32, name="junk", tag="junk", bufs=3)
-            nc.scalar.activation(out=junk[:], in_=bank[:], func=ACT.Square, accum_out=accs[:, ic, k : k + 1])
+        pb = []
 
-        def split_e():
-            nc.vector.tensor_tensor(out=el[:], in0=eT[:], in1=ehT[:], op=ALU.subtract)
-            nc.scalar.copy(out=w2[:, :, :, 0], in_=ehT[:])
-            nc.scalar.mul(out=w2[:, :, :, 1], in_=el[:], mul=2.0)
+        def low_part(c):
+            nc.vector.scalar_tensor_tensor(
+                out=eh2[:, 1, c, :], in0=ehT[:, c, :], scalar=-2.0, in1=e2T[:, c, :], op0=ALU.mult, op1=ALU.add
+            )
 
         def row_constants():
-            nc.vector.tensor_tensor(out=kk[:], in0=w2[:, :, :, 0], in1=w2[:, :, :, 1], op=ALU.add)
-            nc.vector.tensor_tensor(out=kk[:], in0=kk[:], in1=ehT[:], op=ALU.mult)
+            nc.scalar.activation(out=squares[:, 0], in_=e2T[:], func=ACT.Square, scale=0.5)
+            nc.scalar.activation(out=squares[:, 1], in_=eh2[:, 1], func=ACT.Square, scale=0.5)
 
-        def row_constants_sum():
-            kbank = banks.tile([P, 2, 2], F32, name="kbank", tag="bank")
+        def row_constant_sums():
+            kbank = banks.tile([P, 2, 1], F32, name="kbank", tag="bank")
             for ic in range(2):
-                for c in range(4):
-                    nc.tensor.matmul(
-                        out=kbank[:, ic, :],
-                        lhsT=kk[:, c, ic * P : (ic + 1) * P],
-                        rhs=ones[:],
-                        start=(c == 0),
-                        stop=(c == 3),
-                    )
-            nc.vector.tensor_copy(out=ki[:], in_=kbank[:, :, 0])
+                for s in range(2):
+                    for c in range(4):
+                        nc.tensor.matmul(
+                            out=kbank[:, ic, :],
+                            lhsT=squares[:, s, c, ic * P : (ic + 1) * P],
+                            rhs=signs[:, s : s + 1],
+                            start=(s == 0 and c == 0),
+                            stop=(s == 1 and c == 3),
+                        )
+            nc.scalar.copy(out=ki[:], in_=kbank[:, :, 0])
 
         def turn_positives():
-            pb = banks.tile([P, 4, B], BF16, name="pb", tag="bank")
+            pb.append(banks.tile([P, 4, B], BF16, name="pb", tag="bank"))
             for c in range(4):
                 for ic in range(2):
                     lo = ic * EMB + c * P
                     nc.tensor.transpose(
-                        out=pb[:, c, ic * P : (ic + 1) * P], in_=praw[:, lo : lo + P], identity=ident_b[:]
+                        out=pb[0][:, c, ic * P : (ic + 1) * P], in_=praw[:, lo : lo + P], identity=ident_b[:]
                     )
-            nc.scalar.copy(out=pT[:], in_=pb[:])
 
-        def positives_diff():
-            nc.vector.tensor_tensor(out=rp[:], in0=pT[:], in1=eT[:], op=ALU.subtract)
-            nc.vector.tensor_scalar_max(out=rp[:], in0=rp[:], scalar1=0.0)
+        def positives_diff(c):
+            nc.vector.scalar_tensor_tensor(
+                out=rp[:, c, :], in0=e2T[:, c, :], scalar=-0.5, in1=pb[0][:, c, :], op0=ALU.mult, op1=ALU.add
+            )
 
-        def positives_sum():
+        def positives_relu():
+            nc.scalar.activation(out=rp[:], in_=rp[:], func=ACT.Relu)
+
+        def positives_sums():
             for ic in range(2):
                 bank = turn_into_bank([rp[:, c, ic * P : (ic + 1) * P] for c in range(4)])
-                junk = mpool.tile([P, EMB], F32, name="junk", tag="junk", bufs=3)
-                nc.scalar.activation(out=junk[:], in_=bank[:], func=ACT.Square, accum_out=psum_sq[:, ic : ic + 1])
+                square_sum(bank[:], psum_sq[:, ic : ic + 1])
+
+        def negative_norms():
+            for jc in range(4):
+                square_sum(nraw[:, jc * EMB : (jc + 1) * EMB], nn[:, jc : jc + 1])
 
         def finish_store(ic):
             rows = slice(ic * P, (ic + 1) * P)
-            bank = turn_into_bank([uj[:, jc, rows] for jc in range(3)])
+            bank = turn_into_bank([uj[:, jc, rows] for jc in range(4)])
             res = fin.tile([P, NNEG + 1], F32, name="res%d" % ic)
             nc.scalar.activation(out=res[:, 0:1], in_=psum_sq[:, ic : ic + 1], func=ACT.Sqrt)
-            nc.scalar.activation(out=res[:, NV + 1 : NNEG + 1], in_=accs[:, ic, :], func=ACT.Sqrt)
-            nc.vector.tensor_tensor(out=qs[:, ic, :], in0=bank[:, 0:NV], in1=qs[:, ic, :], op=ALU.subtract)
+            nc.vector.tensor_tensor(out=qs[:, ic, :], in0=bank[:], in1=qs[:, ic, :], op=ALU.subtract)
             nc.vector.tensor_scalar(
                 out=qs[:, ic, :], in0=qs[:, ic, :], scalar1=ki[:, ic : ic + 1], scalar2=0.0, op0=ALU.add, op1=ALU.max
             )
-            nc.scalar.activation(out=res[:, 1 : NV + 1], in_=qs[:, ic, :], func=ACT.Sqrt)
+            nc.scalar.activation(out=res[:, 1 : NNEG + 1], in_=qs[:, ic, :], func=ACT.Sqrt)
             nc.vector.tensor_scalar_mul(out=res[:], in0=res[:], scalar1=-1.0)
             nc.sync.dma_start(out=out[rows, :], in_=res[:])
 
-        q_state = {}
-        a_state = {}
-        spare = []
-
-        def min_step(j):
-            h, col = divmod(j, NV // 2)
-            min_row(j)
-            if col == 0:
-                q_state[h] = sbanks.tile([P, 2, NV // 2], F32, name="qbank", tag="qbank")
-            return lambda: min_sums(j, h, col)
-
-        def min_sums(j, h, col):
-            sum_min(j, q_state[h], col)
-            if col == NV // 2 - 1:
-                nc.scalar.copy(out=qs[:, :, (NV // 2) * h : (NV // 2) * (h + 1)], in_=q_state[h][:])
-
-        def max_step(i):
-            g, col = divmod(i, 64)
-            max_row(i)
-            return lambda: max_sums(i, g, col)
-
-        def open_abank(g):
-            abank = sbanks.tile([P, 512], F32, name="abank", tag="abank")
-            a_state[g] = abank[:, 0:NV].rearrange("p (j i t) -> p j i t", j=3, i=64, t=2)
-            spare.append(abank[:, 448:512].bitcast(BF16))
-
-        def keep_warm(count):
-            for w in range(count):
-                nc.tensor.transpose(out=spare[-1], in_=ident_b[:], identity=ident_b[:])
-
-        def max_sums(i, g, col):
-            sum_max(i, a_state[g], col)
-            if col == 63:
-                if g < 3:
-                    open_abank(g + 1)
-                cols = slice(64 * g, 64 * (g + 1))
-                nc.vector.tensor_reduce(out=tj[:, :, cols], in_=a_state[g], axis=mybir.AxisListType.X, op=ALU.add)
-                for jc in range(3):
-                    nc.scalar.activation(
-                        out=uj[:, jc, cols], in_=tj[:, jc, cols], func=ACT.Identity, bias=nn[:, jc : jc + 1], scale=-1.0
-                    )
-
-        open_abank(0)
-        last = None
-        for k in range(NNEG - NV + ROWS_LATE + 1):
-            if k < NNEG - NV:
-                scalar_relu(k)
-            units = []
-            if k < NNEG - NV:
-                units += [(min_step, 3 * k + t) for t in range(3)]
-            if 0 <= k - ROWS_LATE < NNEG - NV:
-                units += [(max_step, 2 * (k - ROWS_LATE) + t) for t in range(2)]
-            for turn, (step, index) in enumerate(units):
-                sums = step(index)
-                if last is not None:
-                    last()
-                last = sums
-                if 0 <= k - 1 < NNEG - NV and turn < 2:
-                    scalar_square(k - 1, turn)
-                keep_warm(2 if turn in (2, 4) else 1)
-            if k == 0:
-                split_e()
-            if k == 6:
-                row_constants()
-            if k == 8:
-                turn_positives()
-            if k == 10:
-                positives_diff()
-            if k == 14:
-                row_constants_sum()
-                positives_sum()
-            if k == 18:
-                negative_norms()
-        last()
-        finish_store(0)
+        steps = [(min_row, min_sums, j) for j in range(NNEG)] + [(max_row, max_sums, i) for i in range(B)]
+        side = {
+            40: turn_positives,
+            56: positives_relu,
+            64: positives_sums,
+            72: negative_norms,
+            84: row_constants,
+            96: row_constant_sums,
+            NNEG + 140: lambda: finish_store(0),
+        }
+        for c in range(4):
+            side[20 + 4 * c] = lambda c=c: low_part(c)
+            side[44 + 2 * c] = lambda c=c: positives_diff(c)
+        for h in range(2):
+            side[NNEG // 2 * (h + 1) + OUT_LATE] = lambda h=h: min_out(h)
+        for g in range(4):
+            side[NNEG + 64 * (g + 1) + OUT_LATE] = lambda g=g: max_out(g)
+        for s in range(len(steps) + OUT_LATE + 1):
+            if s < len(steps):
+                steps[s][0](steps[s][2])
+            if 0 < s <= len(steps):
+                steps[s - 1][1](steps[s - 1][2])
+            if s in side:
+                side[s]()
         finish_store(1)

@@ -16,8 +16,10 @@ B, NNEG, VF, HID, EMB = 256, 512, 4096, 2048, 512
 FLOPS = 2 * B * VF * HID + 2 * B * HID * EMB + 4 * B * (NNEG + 1) * EMB
 
 W_BUFS = 8
-M_BUFS = 8
-OUT_LATE = 4
+M_BUFS = 4
+OUT_LATE = 2
+Q_GROUP = 4
+M_GROUP = 2
 ROUND_ON_VECTOR = (3, 6, 7)
 
 
@@ -280,10 +282,6 @@ def tile_hypernymvisual_acc_kernel(tc, vfs, p_lfs, n_lfs, W_hidden, b_hidden, W_
         sbanks = ctx.enter_context(tc.psum_pool(name="sbanks", bufs=2))
         wpool = ctx.enter_context(tc.psum_pool(name="wpool", bufs=1))
 
-        signs = fin.tile([P, 2], F32)
-        nc.vector.memset(signs[:, 0:1], 1.0)
-        nc.vector.memset(signs[:, 1:2], -1.0)
-        squares = fin.tile([P, 2, 4, B], F32)
         ki = fin.tile([P, 2], F32)
         rp = fin.tile([P, 4, B], F32)
         nn = fin.tile([P, 4], F32)
@@ -303,59 +301,67 @@ def tile_hypernymvisual_acc_kernel(tc, vfs, p_lfs, n_lfs, W_hidden, b_hidden, W_
                 nc.tensor.transpose(out=bank[:, c * P : (c + 1) * P], in_=pieces[c], identity=ident_f[:])
             return bank
 
-        def square_sum(src, dst):
+        def square_sum(src, dst, scale=1.0):
             junk = mpool.tile([P, EMB], F32, name="junk", tag="junk", bufs=2)
-            nc.scalar.activation(out=junk[:], in_=src, func=ACT.Square, accum_out=dst)
+            nc.scalar.activation(out=junk[:], in_=src, func=ACT.Square, scale=scale, accum_out=dst)
 
         q_tiles = {}
         m_tiles = {}
         q_banks = {}
         a_banks = {}
 
-        def min_row(j):
-            q = mpool.tile([P, 4, B], BF16, name="q", tag="q")
-            for c in range(4):
-                nc.vector.tensor_scalar_min(out=q[:, c, :], in0=ehT[:, c, :], scalar1=nT[:, c, j : j + 1])
-            q_tiles[j] = q
-
-        def min_sums(j):
-            h, col = divmod(j, NNEG // 2)
-            if col == 0:
-                q_banks[h] = sbanks.tile([P, 2, NNEG // 2], F32, name="qbank", tag="sbank")
-            for ic in range(2):
+        def min_rows(u):
+            q = mpool.tile([P, Q_GROUP, 4, B], BF16, name="q", tag="q")
+            for t in range(Q_GROUP):
+                j = Q_GROUP * u + t
                 for c in range(4):
-                    nc.tensor.matmul(
-                        out=q_banks[h][:, ic, col : col + 1],
-                        lhsT=q_tiles[j][:, c, ic * P : (ic + 1) * P],
-                        rhs=nT[:, c, j : j + 1],
-                        start=(c == 0),
-                        stop=(c == 3),
-                    )
-            keep_warm(1 + j % 2)
+                    nc.vector.tensor_scalar_min(out=q[:, t, c, :], in0=ehT[:, c, :], scalar1=nT[:, c, j : j + 1])
+            q_tiles[u] = q
+
+        def min_sums(u):
+            for t in range(Q_GROUP):
+                j = Q_GROUP * u + t
+                h, col = divmod(j, NNEG // 2)
+                if col == 0:
+                    q_banks[h] = sbanks.tile([P, 2, NNEG // 2], F32, name="qbank", tag="sbank")
+                for ic in range(2):
+                    for c in range(4):
+                        nc.tensor.matmul(
+                            out=q_banks[h][:, ic, col : col + 1],
+                            lhsT=q_tiles[u][:, t, c, ic * P : (ic + 1) * P],
+                            rhs=nT[:, c, j : j + 1],
+                            start=(c == 0),
+                            stop=(c == 3),
+                        )
+                keep_warm(1 + j % 2)
 
         def min_out(h):
             nc.scalar.copy(out=qs[:, :, (NNEG // 2) * h : (NNEG // 2) * (h + 1)], in_=q_banks[h][:])
 
-        def max_row(i):
-            m = mpool.tile([P, 4, NNEG], BF16, name="m", tag="m")
-            for c in range(4):
-                nc.vector.tensor_scalar_max(out=m[:, c, :], in0=nT[:, c, :], scalar1=ehT[:, c, i : i + 1])
-            m_tiles[i] = m
-
-        def max_sums(i):
-            g, col = divmod(i, 64)
-            if col == 0:
-                a_banks[g] = sbanks.tile([P, 4, 64, 2], F32, name="abank", tag="sbank")
-            for jc in range(4):
+        def max_rows(u):
+            m = mpool.tile([P, M_GROUP, 4, NNEG], BF16, name="m", tag="m")
+            for t in range(M_GROUP):
+                i = M_GROUP * u + t
                 for c in range(4):
-                    nc.tensor.matmul(
-                        out=a_banks[g][:, jc, col, :],
-                        lhsT=m_tiles[i][:, c, jc * P : (jc + 1) * P],
-                        rhs=eh2[:, :, c, i],
-                        start=(c == 0),
-                        stop=(c == 3),
-                    )
-            keep_warm(3)
+                    nc.vector.tensor_scalar_max(out=m[:, t, c, :], in0=nT[:, c, :], scalar1=ehT[:, c, i : i + 1])
+            m_tiles[u] = m
+
+        def max_sums(u):
+            for t in range(M_GROUP):
+                i = M_GROUP * u + t
+                g, col = divmod(i, 64)
+                if col == 0:
+                    a_banks[g] = sbanks.tile([P, 4, 64, 2], F32, name="abank", tag="sbank")
+                for jc in range(4):
+                    for c in range(4):
+                        nc.tensor.matmul(
+                            out=a_banks[g][:, jc, col, :],
+                            lhsT=m_tiles[u][:, t, c, jc * P : (jc + 1) * P],
+                            rhs=eh2[:, :, c, i],
+                            start=(c == 0),
+                            stop=(c == 3),
+                        )
+                keep_warm(3)
 
         def max_out(g):
             cols = slice(64 * g, 64 * (g + 1))
@@ -373,22 +379,9 @@ def tile_hypernymvisual_acc_kernel(tc, vfs, p_lfs, n_lfs, W_hidden, b_hidden, W_
             )
 
         def row_constants():
-            nc.scalar.activation(out=squares[:, 0], in_=e2T[:], func=ACT.Square, scale=0.5)
-            nc.scalar.activation(out=squares[:, 1], in_=eh2[:, 1], func=ACT.Square, scale=0.5)
-
-        def row_constant_sums():
-            kbank = banks.tile([P, 2, 1], F32, name="kbank", tag="bank")
             for ic in range(2):
-                for s in range(2):
-                    for c in range(4):
-                        nc.tensor.matmul(
-                            out=kbank[:, ic, :],
-                            lhsT=squares[:, s, c, ic * P : (ic + 1) * P],
-                            rhs=signs[:, s : s + 1],
-                            start=(s == 0 and c == 0),
-                            stop=(s == 1 and c == 3),
-                        )
-            nc.scalar.copy(out=ki[:], in_=kbank[:, :, 0])
+                bank = turn_into_bank([e2T[:, c, ic * P : (ic + 1) * P] for c in range(4)])
+                square_sum(bank[:], ki[:, ic : ic + 1], scale=0.5)
 
         def turn_positives():
             pb.append(banks.tile([P, 4, B], BF16, name="pb", tag="bank"))
@@ -429,24 +422,25 @@ def tile_hypernymvisual_acc_kernel(tc, vfs, p_lfs, n_lfs, W_hidden, b_hidden, W_
             nc.vector.tensor_scalar_mul(out=res[:], in0=res[:], scalar1=-1.0)
             nc.sync.dma_start(out=out[rows, :], in_=res[:])
 
-        steps = [(min_row, min_sums, j) for j in range(NNEG)] + [(max_row, max_sums, i) for i in range(B)]
+        half = NNEG // Q_GROUP
+        steps = [(min_rows, min_sums, u) for u in range(half)]
+        steps += [(max_rows, max_sums, u) for u in range(B // M_GROUP)]
         side = {
-            40: turn_positives,
-            56: positives_relu,
-            64: positives_sums,
-            72: negative_norms,
-            84: row_constants,
-            96: row_constant_sums,
-            NNEG + 140: lambda: finish_store(0),
+            10: turn_positives,
+            16: positives_relu,
+            18: positives_sums,
+            20: negative_norms,
+            24: row_constants,
+            half + 75: lambda: finish_store(0),
         }
         for c in range(4):
-            side[20 + 4 * c] = lambda c=c: low_part(c)
-            side[44 + 2 * c] = lambda c=c: positives_diff(c)
+            side[4 + c] = lambda c=c: low_part(c)
+            side[11 + c] = lambda c=c: positives_diff(c)
         for h in range(2):
-            side[NNEG // 2 * (h + 1) + OUT_LATE] = lambda h=h: min_out(h)
+            side[half // 2 * (h + 1) + OUT_LATE] = lambda h=h: min_out(h)
         for g in range(4):
-            side[NNEG + 64 * (g + 1) + OUT_LATE] = lambda g=g: max_out(g)
-        for s in range(len(steps) + OUT_LATE + 1):
+            side[half + 64 // M_GROUP * (g + 1) + OUT_LATE - (g == 3)] = lambda g=g: max_out(g)
+        for s in range(len(steps) + OUT_LATE):
             if s < len(steps):
                 steps[s][0](steps[s][2])
             if 0 < s <= len(steps):

from contextlib import ExitStack

import concourse.mybir as mybir
from concourse.masks import make_identity

F32 = mybir.dt.float32
BF16 = mybir.dt.bfloat16
U32 = mybir.dt.uint32
U8 = mybir.dt.uint8
FP8X4 = mybir.dt.float8_e4m3fn_x4
ALU = mybir.AluOpType
ACT = mybir.ActivationFunctionType

P = 128
B, NNEG, VF, HID, EMB = 256, 512, 4096, 2048, 512
FLOPS = 2 * B * VF * HID + 2 * B * HID * EMB + 4 * B * (NNEG + 1) * EMB

W_BUFS = 8
M_BUFS = 4
OUT_LATE = 2
Q_GROUP = 4
M_GROUP = 2
ROUND_ON_VECTOR = (3, 6, 7)


def tile_hypernymvisual_acc_kernel(tc, vfs, p_lfs, n_lfs, W_hidden, b_hidden, W_embed, b_embed, out):
    nc = tc.nc
    with ExitStack() as ctx:
        ctx.enter_context(tc.manual_schedule())
        keep = ctx.enter_context(tc.tile_pool(name="keep", bufs=1))
        ident_f = keep.tile([P, P], F32)
        make_identity(nc, ident_f[:])
        ident_b = keep.tile([P, P], BF16)
        make_identity(nc, ident_b[:])
        nT = keep.tile([P, 4, NNEG], BF16)
        e2T = keep.tile([P, 4, B], F32)
        eh2 = keep.tile([P, 2, 4, B], BF16)
        ehT = eh2[:, 0]
        bias2 = keep.tile([P, 4], F32)
        nraw = keep.tile([P, 4 * EMB], BF16)
        bias = keep.tile([P, 3, 8], F32)
        one = keep.tile([P, 1], F32)
        nc.vector.memset(one[:], 1.0)
        warm = keep.tile([P, 1], F32)

        praw = keep.tile([P, 2 * EMB], BF16)

        with ExitStack() as mx:
            fix = mx.enter_context(tc.tile_pool(name="fix", bufs=1))
            raws = mx.enter_context(tc.tile_pool(name="raws", bufs=W_BUFS))
            work = mx.enter_context(tc.tile_pool(name="work", bufs=4))
            ps_t = mx.enter_context(tc.psum_pool(name="ps_t", bufs=6))
            ps_a = mx.enter_context(tc.psum_pool(name="ps_a", bufs=2))

            def copy_out(on_vector, dst, src):
                if on_vector:
                    nc.vector.tensor_copy(out=dst, in_=src)
                else:
                    nc.scalar.copy(out=dst, in_=src)

            brow = fix.tile([P, 3 * P], BF16)
            nc.vector.memset(brow[:], 0.0)
            nc.scalar.dma_start(out=brow[0:8, 0 : 2 * P], in_=b_hidden.rearrange("(r c) -> r c", c=2 * P))
            nc.scalar.dma_start(out=brow[0:4, 2 * P : 3 * P], in_=b_embed.rearrange("(r c) -> r c", c=P))
            nc.scalar.activation(out=warm[:], in_=one[:], func=ACT.Sqrt)
            vraw = []
            for bc in range(2):
                t = fix.tile([P, VF], BF16, name="vraw%d" % bc)
                for half in range(2):
                    cols = slice(half * VF // 2, (half + 1) * VF // 2)
                    nc.sync.dma_start(out=t[:, cols], in_=vfs[bc * P : (bc + 1) * P, cols])
                vraw.append(t)
            weraw = fix.tile([P, 4 * HID], BF16)
            wraws = []
            w_rows = W_hidden.rearrange("(g u m e) k -> g u e m k", g=4, u=2, m=P, e=2)

            def load_w(hc):
                t = raws.tile([P, VF], BF16, name="wraw", tag="wraw")
                nc.sync.dma_start(out=t[:], in_=w_rows[hc // 4, (hc // 2) % 2, hc % 2])
                wraws.append(t)

            for hc in range(W_BUFS):
                load_w(hc)

            def load_side():
                nc.sync.dma_start(
                    out=weraw[:].rearrange("p (c k) -> p c k", c=4), in_=W_embed.rearrange("(c p) k -> p c k", p=P)
                )
                nc.sync.dma_start(
                    out=nraw[:].rearrange("p (c k) -> p c k", c=4), in_=n_lfs.rearrange("(c p) k -> p c k", p=P)
                )
                nc.sync.dma_start(
                    out=praw[:].rearrange("p (c k) -> p c k", c=2), in_=p_lfs.rearrange("(c p) k -> p c k", p=P)
                )

            def turn_words(words, banks_of, dst_of_q, vector_banks, first_bank):
                for q in banks_of:
                    xt = ps_t.tile([P, 2, 2, P], F32, name="xt", tag="xt")
                    for gg in range(2):
                        for u in range(2):
                            lo = 256 * (2 * q + gg) + P * u
                            nc.tensor.transpose(out=xt[:, gg, u, :], in_=words[:, lo : lo + P], identity=ident_f[:])
                    copy_out((first_bank + q) in vector_banks, dst_of_q(q), xt[:].rearrange("p g u r -> p g r u"))

            vgrp = fix.tile([P, 8 * B * 4], BF16, align_bytes=64)
            vgrp_w = vgrp[:].bitcast(F32).rearrange("p (g r u) -> p g r u", g=8, r=B, u=2)
            vcodes = fix.tile([P, 8 * B], U32, align_bytes=64)
            vscales = fix.tile([P, 8 * B], U8, align_bytes=64)
            for bc in range(2):
                turn_words(
                    vraw[bc][:].bitcast(F32),
                    range(4),
                    lambda q: vgrp_w[:, 2 * q : 2 * q + 2, bc * P : (bc + 1) * P, :],
                    (0, 2, 4, 6),
                    4 * bc,
                )

            def quantise_v(h):
                nc.vector.quantize_mx(
                    out=vcodes[:, 1024 * h : 1024 * (h + 1)].bitcast(FP8X4),
                    scales=vscales[:, 1024 * h : 1024 * (h + 1)],
                    in_=vgrp[:, 4096 * h : 4096 * (h + 1)],
                )

            hgrp = fix.tile([P, 4 * B * 4], BF16, align_bytes=64)
            hgrp_v = hgrp[:].rearrange("p (g b t) -> p g b t", g=4, b=B, t=4)
            hcodes = fix.tile([P, 4 * B], U32, align_bytes=64)
            hscales = fix.tile([P, 4 * B], U8, align_bytes=64)
            egrp = fix.tile([P, 4 * EMB * 4], BF16, align_bytes=64)
            egrp_w = egrp[:].bitcast(F32).rearrange("p (g d u) -> p g d u", g=4, d=EMB, u=2)
            ecodes = fix.tile([P, 4 * EMB], U32, align_bytes=64)
            escales = fix.tile([P, 4 * EMB], U8, align_bytes=64)

            def turn_bias():
                bt = ps_t.tile([P, 3, P], BF16, name="bt", tag="xt")
                for e in range(2):
                    nc.tensor.transpose(out=bt[:, e, :], in_=brow[:, e : 2 * P : 2], identity=ident_b[:])
                nc.tensor.transpose(out=bt[:, 2, :], in_=brow[:, 2 * P : 3 * P], identity=ident_b[:])
                nc.vector.tensor_copy(out=bias[:], in_=bt[:, :, 0:8])
                nc.vector.tensor_scalar_mul(out=bias2[:], in0=bt[:, 2, 0:4], scalar1=2.0)

            def turn_embed(dc):
                turn_words(
                    weraw[:, dc * HID : (dc + 1) * HID].bitcast(F32),
                    range(2),
                    lambda q: egrp_w[:, 2 * q : 2 * q + 2, dc * P : (dc + 1) * P, :],
                    (1, 3),
                    0,
                )

            def turn_negatives():
                for ch in range(2):
                    nb = ps_t.tile([P, 2, NNEG], BF16, name="nb", tag="xt")
                    for cc in range(2):
                        for jc in range(4):
                            lo = jc * EMB + (2 * ch + cc) * P
                            nc.tensor.transpose(
                                out=nb[:, cc, jc * P : (jc + 1) * P], in_=nraw[:, lo : lo + P], identity=ident_b[:]
                            )
                    copy_out(False, nT[:, 2 * ch : 2 * ch + 2, :], nb[:])

            def quantise_embed(h):
                nc.vector.quantize_mx(
                    out=ecodes[:, 1024 * h : 1024 * (h + 1)].bitcast(FP8X4),
                    scales=escales[:, 1024 * h : 1024 * (h + 1)],
                    in_=egrp[:, 4096 * h : 4096 * (h + 1)],
                )

            wgrps = {}
            wq = {}

            def turn_w(hc):
                wgrp = work.tile([P, VF], BF16, name="wgrp", tag="wgrp", bufs=3, align_bytes=64)
                wgrp_w = wgrp[:].bitcast(F32).rearrange("p (g r u) -> p g r u", g=8, r=P, u=2)
                turn_words(
                    wraws[hc][:].bitcast(F32),
                    range(4),
                    lambda q: wgrp_w[:, 2 * q : 2 * q + 2, :, :],
                    ROUND_ON_VECTOR,
                    4 * (hc % 2),
                )
                wgrps[hc] = wgrp
                if hc + W_BUFS < 16:
                    load_w(hc + W_BUFS)
                    if hc + W_BUFS == 15:
                        load_side()

            def quantise_w(hc):
                wcodes = work.tile([P, 1024], U32, name="wcodes", tag="wcodes", align_bytes=64)
                wscales = work.tile([P, 1024], U8, name="wscales", tag="wscales", align_bytes=64)
                nc.vector.quantize_mx(out=wcodes[:].bitcast(FP8X4), scales=wscales[:], in_=wgrps[hc][:])
                wq[hc] = (wcodes, wscales)

            def layer1(hc):
                wcodes, wscales = wq[hc]
                acc = ps_a.tile([P, B], F32, name="acc", tag="acc")
                for g in range(8):
                    nc.tensor.matmul_mx(
                        out=acc[:],
                        lhsT=wcodes[:, P * g : P * (g + 1)].bitcast(FP8X4),
                        lhsT_scale=wscales[:, P * g : P * (g + 1)],
                        rhs=vcodes[:, B * g : B * (g + 1)].bitcast(FP8X4),
                        rhs_scale=vscales[:, B * g : B * (g + 1)],
                        start=(g == 0),
                        stop=(g == 7),
                    )
                nc.scalar.activation(
                    out=hgrp_v[:, hc // 4, :, hc % 4],
                    in_=acc[:],
                    func=ACT.Identity,
                    bias=bias[:, hc % 2, hc // 2 : hc // 2 + 1],
                    scale=1.0,
                )

            def quantise_h(g2):
                nc.vector.quantize_mx(
                    out=hcodes[:, B * g2 : B * (g2 + 1)].bitcast(FP8X4),
                    scales=hscales[:, B * g2 : B * (g2 + 1)],
                    in_=hgrp[:, 4 * B * g2 : 4 * B * (g2 + 1)],
                )

            quantise_v(0)
            turn_w(0)
            quantise_v(1)
            quantise_w(0)
            turn_bias()
            for hc in range(1, 4):
                turn_w(hc)
                layer1(hc - 1)
                quantise_w(hc)
            for rnd in range(2, 8):
                if rnd == 7:
                    for dc in range(4):
                        turn_embed(dc)
                turn_w(2 * rnd)
                turn_w(2 * rnd + 1)
                if rnd == 2:
                    layer1(3)
                else:
                    layer1(2 * rnd - 2)
                    layer1(2 * rnd - 1)
                quantise_w(2 * rnd)
                quantise_w(2 * rnd + 1)
                if rnd == 3:
                    quantise_h(0)
                if rnd == 5:
                    quantise_h(1)
                if rnd == 7:
                    quantise_embed(0)
                    quantise_embed(1)
                    quantise_h(2)
            turn_negatives()
            layer1(14)
            layer1(15)
            quantise_h(3)

            accs2 = [ps_t.tile([P, B], F32, name="acc2", tag="xt") for dc in range(4)]
            for g2 in range(4):
                for dc in range(4):
                    lo = EMB * g2 + P * dc
                    nc.tensor.matmul_mx(
                        out=accs2[dc][:],
                        lhsT=ecodes[:, lo : lo + P].bitcast(FP8X4),
                        lhsT_scale=escales[:, lo : lo + P],
                        rhs=hcodes[:, B * g2 : B * (g2 + 1)].bitcast(FP8X4),
                        rhs_scale=hscales[:, B * g2 : B * (g2 + 1)],
                        start=(g2 == 0),
                        stop=(g2 == 3),
                    )
            first_warm = ps_a.tile([P, P], BF16, name="first_warm", tag="acc")
            for w in range(20):
                nc.tensor.transpose(out=first_warm[:], in_=ident_b[:], identity=ident_b[:])
            for dc in range(4):
                nc.vector.tensor_scalar_add(out=ehT[:, dc, :], in0=accs2[dc][:], scalar1=bias[:, 2, dc : dc + 1])
                nc.scalar.activation(
                    out=e2T[:, dc, :], in_=accs2[dc][:], func=ACT.Identity, bias=bias2[:, dc : dc + 1], scale=2.0
                )

        fin = ctx.enter_context(tc.tile_pool(name="fin", bufs=1))
        mpool = ctx.enter_context(tc.tile_pool(name="mpool", bufs=M_BUFS))
        banks = ctx.enter_context(tc.psum_pool(name="banks", bufs=4))
        sbanks = ctx.enter_context(tc.psum_pool(name="sbanks", bufs=2))
        wpool = ctx.enter_context(tc.psum_pool(name="wpool", bufs=1))

        ki = fin.tile([P, 2], F32)
        rp = fin.tile([P, 4, B], F32)
        nn = fin.tile([P, 4], F32)
        psum_sq = fin.tile([P, 2], F32)
        qs = fin.tile([P, 2, NNEG], F32)
        tj = fin.tile([P, 4, B], F32)
        uj = fin.tile([P, 4, B], F32)
        wbank = wpool.tile([P, 4, P], BF16)

        def keep_warm(count):
            for w in range(count):
                nc.tensor.transpose(out=wbank[:, w % 4, :], in_=ident_b[:], identity=ident_b[:])

        def turn_into_bank(pieces):
            bank = banks.tile([P, 4 * P], F32, name="bank", tag="bank")
            for c in range(4):
                nc.tensor.transpose(out=bank[:, c * P : (c + 1) * P], in_=pieces[c], identity=ident_f[:])
            return bank

        def square_sum(src, dst, scale=1.0):
            junk = mpool.tile([P, EMB], F32, name="junk", tag="junk", bufs=2)
            nc.scalar.activation(out=junk[:], in_=src, func=ACT.Square, scale=scale, accum_out=dst)

        q_tiles = {}
        m_tiles = {}
        q_banks = {}
        a_banks = {}

        def min_rows(u):
            q = mpool.tile([P, Q_GROUP, 4, B], BF16, name="q", tag="q")
            for t in range(Q_GROUP):
                j = Q_GROUP * u + t
                for c in range(4):
                    nc.vector.tensor_scalar_min(out=q[:, t, c, :], in0=ehT[:, c, :], scalar1=nT[:, c, j : j + 1])
            q_tiles[u] = q

        def min_sums(u):
            for t in range(Q_GROUP):
                j = Q_GROUP * u + t
                h, col = divmod(j, NNEG // 2)
                if col == 0:
                    q_banks[h] = sbanks.tile([P, 2, NNEG // 2], F32, name="qbank", tag="sbank")
                for ic in range(2):
                    for c in range(4):
                        nc.tensor.matmul(
                            out=q_banks[h][:, ic, col : col + 1],
                            lhsT=q_tiles[u][:, t, c, ic * P : (ic + 1) * P],
                            rhs=nT[:, c, j : j + 1],
                            start=(c == 0),
                            stop=(c == 3),
                        )
                keep_warm(1 + j % 2)

        def min_out(h):
            nc.scalar.copy(out=qs[:, :, (NNEG // 2) * h : (NNEG // 2) * (h + 1)], in_=q_banks[h][:])

        def max_rows(u):
            m = mpool.tile([P, M_GROUP, 4, NNEG], BF16, name="m", tag="m")
            for t in range(M_GROUP):
                i = M_GROUP * u + t
                for c in range(4):
                    nc.vector.tensor_scalar_max(out=m[:, t, c, :], in0=nT[:, c, :], scalar1=ehT[:, c, i : i + 1])
            m_tiles[u] = m

        def max_sums(u):
            for t in range(M_GROUP):
                i = M_GROUP * u + t
                g, col = divmod(i, 64)
                if col == 0:
                    a_banks[g] = sbanks.tile([P, 4, 64, 2], F32, name="abank", tag="sbank")
                for jc in range(4):
                    for c in range(4):
                        nc.tensor.matmul(
                            out=a_banks[g][:, jc, col, :],
                            lhsT=m_tiles[u][:, t, c, jc * P : (jc + 1) * P],
                            rhs=eh2[:, :, c, i],
                            start=(c == 0),
                            stop=(c == 3),
                        )
                keep_warm(3)

        def max_out(g):
            cols = slice(64 * g, 64 * (g + 1))
            nc.vector.tensor_reduce(out=tj[:, :, cols], in_=a_banks[g][:], axis=mybir.AxisListType.X, op=ALU.add)
            for jc in range(4):
                nc.scalar.activation(
                    out=uj[:, jc, cols], in_=tj[:, jc, cols], func=ACT.Identity, bias=nn[:, jc : jc + 1], scale=-1.0
                )

        pb = []

        def low_part(c):
            nc.vector.scalar_tensor_tensor(
                out=eh2[:, 1, c, :], in0=ehT[:, c, :], scalar=-2.0, in1=e2T[:, c, :], op0=ALU.mult, op1=ALU.add
            )

        def row_constants():
            for ic in range(2):
                bank = turn_into_bank([e2T[:, c, ic * P : (ic + 1) * P] for c in range(4)])
                square_sum(bank[:], ki[:, ic : ic + 1], scale=0.5)

        def turn_positives():
            pb.append(banks.tile([P, 4, B], BF16, name="pb", tag="bank"))
            for c in range(4):
                for ic in range(2):
                    lo = ic * EMB + c * P
                    nc.tensor.transpose(
                        out=pb[0][:, c, ic * P : (ic + 1) * P], in_=praw[:, lo : lo + P], identity=ident_b[:]
                    )

        def positives_diff(c):
            nc.vector.scalar_tensor_tensor(
                out=rp[:, c, :], in0=e2T[:, c, :], scalar=-0.5, in1=pb[0][:, c, :], op0=ALU.mult, op1=ALU.add
            )

        def positives_relu():
            nc.scalar.activation(out=rp[:], in_=rp[:], func=ACT.Relu)

        def positives_sums():
            for ic in range(2):
                bank = turn_into_bank([rp[:, c, ic * P : (ic + 1) * P] for c in range(4)])
                square_sum(bank[:], psum_sq[:, ic : ic + 1])

        def negative_norms():
            for jc in range(4):
                square_sum(nraw[:, jc * EMB : (jc + 1) * EMB], nn[:, jc : jc + 1])

        def finish_store(ic):
            rows = slice(ic * P, (ic + 1) * P)
            bank = turn_into_bank([uj[:, jc, rows] for jc in range(4)])
            res = fin.tile([P, NNEG + 1], F32, name="res%d" % ic)
            nc.scalar.activation(out=res[:, 0:1], in_=psum_sq[:, ic : ic + 1], func=ACT.Sqrt)
            nc.vector.tensor_tensor(out=qs[:, ic, :], in0=bank[:], in1=qs[:, ic, :], op=ALU.subtract)
            nc.vector.tensor_scalar(
                out=qs[:, ic, :], in0=qs[:, ic, :], scalar1=ki[:, ic : ic + 1], scalar2=0.0, op0=ALU.add, op1=ALU.max
            )
            nc.scalar.activation(out=res[:, 1 : NNEG + 1], in_=qs[:, ic, :], func=ACT.Sqrt)
            nc.vector.tensor_scalar_mul(out=res[:], in0=res[:], scalar1=-1.0)
            nc.sync.dma_start(out=out[rows, :], in_=res[:])

        half = NNEG // Q_GROUP
        steps = [(min_rows, min_sums, u) for u in range(half)]
        steps += [(max_rows, max_sums, u) for u in range(B // M_GROUP)]
        side = {
            10: turn_positives,
            16: positives_relu,
            18: positives_sums,
            20: negative_norms,
            24: row_constants,
            half + 75: lambda: finish_store(0),
        }
        for c in range(4):
            side[4 + c] = lambda c=c: low_part(c)
            side[11 + c] = lambda c=c: positives_diff(c)
        for h in range(2):
            side[half // 2 * (h + 1) + OUT_LATE] = lambda h=h: min_out(h)
        for g in range(4):
            side[half + 64 // M_GROUP * (g + 1) + OUT_LATE - (g == 3)] = lambda g=g: max_out(g)
        for s in range(len(steps) + OUT_LATE):
            if s < len(steps):
                steps[s][0](steps[s][2])
            if 0 < s <= len(steps):
                steps[s - 1][1](steps[s - 1][2])
            if s in side:
                side[s]()
        finish_store(1)
